import numpy as np
import ml_dtypes


def mxq(x, axis, fmt="e4m3"):
    dtype, down = {"e4m3": (ml_dtypes.float8_e4m3fn, 7), "e5m2": (ml_dtypes.float8_e5m2, 14)}[fmt]
    v = np.moveaxis(np.asarray(x, np.float32).astype(ml_dtypes.bfloat16).astype(np.float64), axis, -1)
    blocks = v.reshape(v.shape[:-1] + (-1, 32))
    amax = np.abs(blocks).max(-1, keepdims=True)
    byte = np.maximum(np.where(amax > 0, np.frexp(amax)[1] - 1 + 127, 0) - down, 1)
    scale = np.exp2(byte - 127.0)
    codes = (blocks / scale).astype(np.float32).astype(dtype).astype(np.float64)
    return np.moveaxis((codes * scale).reshape(v.shape), -1, axis)


WIDE = False


def mx_kscale(k):
    if not WIDE:
        return np.ones(k)
    levels = np.array([10, -10, 5, -5, 0])
    a = np.random.permutation(np.resize(levels, k // 512 * 4)).reshape(k // 512, 4)
    idx = np.arange(k)
    return np.exp2(a[idx // 512, idx % 128 // 32])


BF16 = ml_dtypes.bfloat16


def bf(x):
    return np.asarray(x, np.float32).astype(BF16)


def f64(x):
    return np.asarray(x).astype(np.float64)


E2M1 = np.array([0.0, 0.5, 1.0, 1.5, 2.0, 3.0, 4.0, 6.0, -0.0, -0.5, -1.0, -1.5, -2.0, -3.0, -4.0, -6.0])


def pack_weight(w, fmt):
    k, n = w.shape
    w = f64(bf(w)).reshape(k // 32, 32, n)
    amax = np.abs(w).max(1)
    if fmt == "e4m3":
        byte = np.frexp(amax)[1] - 1 + 127 - 7
    else:
        mant, ex = np.frexp(amax / 6.0)
        byte = np.where(mant > 0.5, ex, ex - 1) + 127
    byte = np.clip(np.where(amax > 0, byte, 1), 1, 254)
    scaled = (w * np.exp2(127.0 - byte)[:, None, :]).reshape(k, n).astype(np.float32)
    by_word = np.ascontiguousarray(scaled.reshape(k // 512, 128, 4, n).transpose(0, 1, 3, 2))
    if fmt == "e4m3":
        words = by_word.astype(ml_dtypes.float8_e4m3fn).view(np.uint8)
    else:
        c = by_word.astype(ml_dtypes.float4_e2m1fn).view(np.uint8) & 0xF
        words = c[..., 0::2] | (c[..., 1::2] << 4)
    return np.ascontiguousarray(words), np.ascontiguousarray(byte.astype(np.uint8).reshape(k // 512, 16, n))


def unpack_weight(words, scales, fmt):
    g, p, n, _ = words.shape
    if fmt == "e4m3":
        vals = np.ascontiguousarray(words).view(ml_dtypes.float8_e4m3fn).astype(np.float64)
    else:
        nib = np.empty((g, p, n, 4), np.uint8)
        nib[..., 0::2] = words & 0xF
        nib[..., 1::2] = words >> 4
        vals = E2M1[nib]
    vals = vals * np.repeat(np.exp2(scales.astype(np.float64) - 127.0), 8, axis=1)[..., None]
    return vals.transpose(0, 1, 3, 2).reshape(g * 512, n)


B, IN, G, OUT = 2048, 512, 8, 512
K = IN * G
GRID_MIN, GRID_MAX = -2.0, 2.0
H = (GRID_MAX - GRID_MIN) / (G - 1)


def setup_inputs():
    sf = mx_kscale(K)[::G]
    a = np.log2(sf.max() / sf)
    grid = bf(np.linspace(GRID_MIN, GRID_MAX, G) + 0.02 * np.random.standard_normal(G))
    z = np.random.standard_normal((B, IN))
    far = f64(grid).max() + H * np.sqrt(a * np.log(2.0)) + 0.05 * z
    x = np.where(a > 0, far, z)
    w = np.random.standard_normal((K, OUT)) / np.sqrt(IN) * np.repeat(np.exp2(a), G)[:, None]
    words, scales = pack_weight(w, "e4m3")
    return {"x": bf(x), "grid": grid, "spline_weight_words": words, "spline_weight_scales": scales}


def reference(x, grid, spline_weight_words, spline_weight_scales):
    h = (GRID_MAX - GRID_MIN) / (G - 1)
    basis = np.exp(-np.square((f64(x)[..., None] - f64(grid)) / h))
    return mxq(basis.reshape(basis.shape[0], -1), 1, "e4m3") @ unpack_weight(spline_weight_words, spline_weight_scales, "e4m3")

@@ -1,0 +1,216 @@
+from contextlib import ExitStack
+
+import concourse.mybir as mybir
+from concourse.masks import make_identity
+
+F32 = mybir.dt.float32
+BF16 = mybir.dt.bfloat16
+I32 = mybir.dt.int32
+U32 = mybir.dt.uint32
+U8 = mybir.dt.uint8
+FP8X4 = mybir.dt.float8_e4m3fn_x4
+ACT = mybir.ActivationFunctionType
+
+P = 128
+PACK = 4
+BATCH, FEATURES, GRID, OUT = 2048, 512, 8, 512
+K_PASS = P * PACK
+PASSES = FEATURES * GRID // K_PASS
+INV_H2 = 49.0 / 16.0
+
+ROW_TILES = BATCH // P
+CHUNK_TILES = 4
+CHUNK = CHUNK_TILES * P
+PAIR = 2
+STEPS_PER_CHUNK = PASSES // PAIR
+STEPS = (ROW_TILES // CHUNK_TILES) * STEPS_PER_CHUNK
+
+SCALAR_COLS = 128
+VECTOR_COLS = CHUNK - SCALAR_COLS
+
+FLOPS = 2 * BATCH * FEATURES * GRID * OUT
+
+
+def tile_gaussiankernel_kernel(tc, x, grid, spline_weight_words, spline_weight_scales, out):
+    nc = tc.nc
+    x_rows = x.rearrange("(p r) i -> p r i", r=ROW_TILES)
+    out_rows = out.rearrange("(p r) n -> p r n", r=ROW_TILES)
+
+    with ExitStack() as ctx:
+        keep = ctx.enter_context(tc.tile_pool(name="keep", bufs=1))
+        xt_pool = ctx.enter_context(tc.tile_pool(name="xt", bufs=3))
+        xr_pool = ctx.enter_context(tc.tile_pool(name="xr", bufs=2))
+        sq_pool = ctx.enter_context(tc.tile_pool(name="sq", bufs=3))
+        basis_pool = ctx.enter_context(tc.tile_pool(name="basis", bufs=2))
+        mx_pool = ctx.enter_context(tc.tile_pool(name="mx", bufs=2))
+        res_pool = ctx.enter_context(tc.tile_pool(name="res", bufs=4))
+        xt_psum = ctx.enter_context(tc.psum_pool(name="xt_psum", bufs=2))
+        xr_psum = ctx.enter_context(tc.psum_pool(name="xr_psum", bufs=2))
+        acc_psum = ctx.enter_context(tc.psum_pool(name="acc_psum", bufs=1))
+        ctx.enter_context(tc.manual_schedule())
+
+        w_scales = keep.tile([P, PASSES, OUT], U8, align_bytes=64)
+        nc.vector.memset(w_scales[:].rearrange("p g n -> p (g n)").bitcast(I32), 0)
+
+        grid_bf = keep.tile([P, PACK], BF16)
+        with nc.allow_non_contiguous_dma(reason="eight bytes of the grid to each partition"):
+            nc.sync.dma_start(out=grid_bf[0:P:2, :], in_=grid[0:PACK].partition_broadcast(P // 2))
+            nc.sync.dma_start(out=grid_bf[1:P:2, :], in_=grid[PACK:GRID].partition_broadcast(P // 2))
+
+        x_sb = keep.tile([P, ROW_TILES, FEATURES], BF16)
+        nc.sync.dma_start(out=x_sb[:, 0:CHUNK_TILES, :], in_=x_rows[:, 0:CHUNK_TILES, :])
+
+        for quad in range(4):
+            nc.sync.dma_start(
+                out=w_scales[32 * quad : 32 * quad + 4, :, :].bitcast(I32),
+                in_=spline_weight_scales[:, 4 * quad : 4 * quad + 4, :].rearrange("g r n -> r g n").bitcast(I32),
+            )
+        w_words = keep.tile([P, PASSES, OUT], U32, align_bytes=64)
+        for g in range(PASSES):
+            nc.sync.dma_start(
+                out=w_words[:, g, :].bitcast(I32),
+                in_=spline_weight_words[g].rearrange("p n t -> p (n t)").bitcast(I32),
+            )
+        for c in range(1, ROW_TILES // CHUNK_TILES):
+            rows = slice(c * CHUNK_TILES, (c + 1) * CHUNK_TILES)
+            nc.sync.dma_start(out=x_sb[:, rows, :], in_=x_rows[:, rows, :])
+
+        ident = keep.tile([P, P], BF16)
+        make_identity(nc, ident[:])
+        spread = keep.tile([P, PAIR, P // 2, 2], BF16)
+        for half in range(PAIR):
+            nc.vector.tensor_copy(
+                out=spread[:, half, :, :],
+                in_=ident[:, 64 * half : 64 * half + 64].unsqueeze(2).to_broadcast([P, P // 2, 2]),
+            )
+        neg_grid = keep.tile([P, PACK], F32)
+        nc.vector.tensor_scalar_mul(out=neg_grid[:], in0=grid_bf[:], scalar1=-1.0)
+
+        xt_ps_of, xt_of, xr_ps_of, xr_of, sq_of, basis_of, codes_of, scales_of, acc_of = {}, {}, {}, {}, {}, {}, {}, {}, {}
+
+        def transpose_features(s):
+            chunk, part = divmod(s, STEPS_PER_CHUNK)
+            xt_ps = xt_psum.tile([P, CHUNK], BF16)
+            for j in range(CHUNK_TILES):
+                nc.tensor.transpose(
+                    xt_ps[:, j * P : (j + 1) * P],
+                    x_sb[:, chunk * CHUNK_TILES + j, part * P : (part + 1) * P],
+                    ident[:],
+                )
+            xt_ps_of[s] = xt_ps
+
+        def copy_transposed(s):
+            xt = xt_pool.tile([P, CHUNK], BF16)
+            nc.scalar.copy(out=xt[:], in_=xt_ps_of[s][:])
+            xt_of[s] = xt
+
+        def spread_features(s):
+            xr_ps = xr_psum.tile([P, PAIR, CHUNK], BF16)
+            xt = xt_of[s]
+            for half in range(PAIR):
+                nc.tensor.matmul(
+                    out=xr_ps[:, half, :],
+                    lhsT=spread[:, half, :, :].rearrange("p i c -> p (i c)"),
+                    rhs=xt[:],
+                    start=True,
+                    stop=True,
+                )
+            xr_ps_of[s] = xr_ps
+
+        def scalar_squares(s):
+            xr_ps = xr_ps_of[s]
+            sq = sq_pool.tile([P, PAIR, PACK, CHUNK], F32)
+            for t in range(PACK):
+                nc.scalar.activation(
+                    out=sq[:, :, t, 0:SCALAR_COLS],
+                    in_=xr_ps[:, :, 0:SCALAR_COLS],
+                    func=ACT.Square,
+                    bias=neg_grid[:, t : t + 1],
+                    scale=1.0,
+                )
+            xr = xr_pool.tile([P, PAIR, VECTOR_COLS], BF16)
+            nc.scalar.copy(out=xr[:], in_=xr_ps[:, :, SCALAR_COLS:CHUNK])
+            sq_of[s] = sq
+            xr_of[s] = xr
+
+        def vector_squares(s):
+            sq = sq_of[s]
+            xr = xr_of[s]
+            for t in range(PACK):
+                nc.vector.tensor_scalar_add(
+                    out=sq[:, :, t, SCALAR_COLS:CHUNK], in0=xr[:], scalar1=neg_grid[:, t : t + 1]
+                )
+            rest = sq[:, :, :, SCALAR_COLS:CHUNK]
+            nc.vector.tensor_mul(out=rest, in0=rest, in1=rest)
+
+        def exponentials(s):
+            sq = sq_of[s]
+            basis = basis_pool.tile([P, PAIR, CHUNK, PACK], BF16, align_bytes=64)
+            for half in range(PAIR):
+                nc.scalar.activation(
+                    out=basis[:, half, :, :].rearrange("p (c i) t -> p c t i", i=4),
+                    in_=sq[:, half, :, :].rearrange("p t (c i) -> p c t i", i=4),
+                    func=ACT.Exp,
+                    scale=-INV_H2,
+                )
+            basis_of[s] = basis
+
+        def quantise(s):
+            basis = basis_of[s]
+            codes = mx_pool.tile([P, PAIR, CHUNK], U32, align_bytes=64)
+            scales = mx_pool.tile([P, PAIR, CHUNK], U8, align_bytes=64)
+            nc.vector.quantize_mx(
+                out=codes[:].rearrange("p h b -> p (h b)").bitcast(FP8X4),
+                scales=scales[:].rearrange("p h b -> p (h b)"),
+                in_=basis[:].rearrange("p h b t -> p (h b t)"),
+            )
+            codes_of[s] = codes
+            scales_of[s] = scales
+
+        def multiply(s):
+            part = s % STEPS_PER_CHUNK
+            codes = codes_of[s]
+            scales = scales_of[s]
+            for j in range(CHUNK_TILES):
+                if part == 0:
+                    acc_of[j] = acc_psum.tile([P, OUT], F32, name="acc_%d" % j, tag="acc_%d" % j)
+                cols = slice(j * P, (j + 1) * P)
+                for half in range(PAIR):
+                    g = part * PAIR + half
+                    nc.tensor.matmul_mx(
+                        out=acc_of[j][:],
+                        lhsT=codes[:, half, cols].bitcast(FP8X4),
+                        lhsT_scale=scales[:, half, cols],
+                        rhs=w_words[:, g, :].bitcast(FP8X4),
+                        rhs_scale=w_scales[:, g, :],
+                        start=(g == 0),
+                        stop=(g == PASSES - 1),
+                    )
+
+        def store_chunk(chunk):
+            for j in range(CHUNK_TILES):
+                res = res_pool.tile([P, OUT], F32)
+                nc.vector.tensor_copy(out=res[:], in_=acc_of[j][:])
+                nc.sync.dma_start(out=out_rows[:, chunk * CHUNK_TILES + j, :], in_=res[:])
+
+        def valid(s):
+            return 0 <= s < STEPS
+
+        for k in range(-4, STEPS + 1):
+            if valid(k + 4):
+                transpose_features(k + 4)
+            if valid(k + 3):
+                spread_features(k + 3)
+            if valid(k):
+                exponentials(k)
+            if valid(k + 1):
+                vector_squares(k + 1)
+            if valid(k + 2):
+                scalar_squares(k + 2)
+            if valid(k + 4):
+                copy_transposed(k + 4)
+            if k > 0 and k % STEPS_PER_CHUNK == 0:
+                store_chunk(k // STEPS_PER_CHUNK - 1)
+            if valid(k):
+                quantise(k)
+                multiply(k)

@@ -58,7 +58,15 @@ def tile_gaussiankernel_kernel(tc, x, grid, spline_weight_words, spline_weight_s
             nc.sync.dma_start(out=grid_bf[1:P:2, :], in_=grid[PACK:GRID].partition_broadcast(P // 2))
 
         x_sb = keep.tile([P, ROW_TILES, FEATURES], BF16)
-        nc.sync.dma_start(out=x_sb[:, 0:CHUNK_TILES, :], in_=x_rows[:, 0:CHUNK_TILES, :])
+
+        def load_x(s):
+            chunk, part = divmod(s, STEPS_PER_CHUNK)
+            rows = slice(chunk * CHUNK_TILES, (chunk + 1) * CHUNK_TILES)
+            cols = slice(part * P, (part + 1) * P)
+            nc.sync.dma_start(out=x_sb[:, rows, cols], in_=x_rows[:, rows, cols])
+
+        for s in range(STEPS_PER_CHUNK):
+            load_x(s)
 
         for quad in range(4):
             nc.sync.dma_start(
@@ -71,9 +79,8 @@ def tile_gaussiankernel_kernel(tc, x, grid, spline_weight_words, spline_weight_s
                 out=w_words[:, g, :].bitcast(I32),
                 in_=spline_weight_words[g].rearrange("p n t -> p (n t)").bitcast(I32),
             )
-        for c in range(1, ROW_TILES // CHUNK_TILES):
-            rows = slice(c * CHUNK_TILES, (c + 1) * CHUNK_TILES)
-            nc.sync.dma_start(out=x_sb[:, rows, :], in_=x_rows[:, rows, :])
+        for s in range(STEPS_PER_CHUNK, STEPS):
+            load_x(s)
 
         ident = keep.tile([P, P], BF16)
         make_identity(nc, ident[:])
@@ -159,11 +166,12 @@ def tile_gaussiankernel_kernel(tc, x, grid, spline_weight_words, spline_weight_s
             basis = basis_of[s]
             codes = mx_pool.tile([P, PAIR, CHUNK], U32, align_bytes=64)
             scales = mx_pool.tile([P, PAIR, CHUNK], U8, align_bytes=64)
-            nc.vector.quantize_mx(
-                out=codes[:].rearrange("p h b -> p (h b)").bitcast(FP8X4),
-                scales=scales[:].rearrange("p h b -> p (h b)"),
-                in_=basis[:].rearrange("p h b t -> p (h b t)"),
-            )
+            for half in range(PAIR):
+                nc.vector.quantize_mx(
+                    out=codes[:, half, :].bitcast(FP8X4),
+                    scales=scales[:, half, :],
+                    in_=basis[:, half, :, :].rearrange("p b t -> p (b t)"),
+                )
             codes_of[s] = codes
             scales_of[s] = scales
 
@@ -171,12 +179,12 @@ def tile_gaussiankernel_kernel(tc, x, grid, spline_weight_words, spline_weight_s
             part = s % STEPS_PER_CHUNK
             codes = codes_of[s]
             scales = scales_of[s]
-            for j in range(CHUNK_TILES):
-                if part == 0:
-                    acc_of[j] = acc_psum.tile([P, OUT], F32, name="acc_%d" % j, tag="acc_%d" % j)
-                cols = slice(j * P, (j + 1) * P)
-                for half in range(PAIR):
-                    g = part * PAIR + half
+            for half in range(PAIR):
+                g = part * PAIR + half
+                for j in range(CHUNK_TILES):
+                    if g == 0:
+                        acc_of[j] = acc_psum.tile([P, OUT], F32, name="acc_%d" % j, tag="acc_%d" % j)
+                    cols = slice(j * P, (j + 1) * P)
                     nc.tensor.matmul_mx(
                         out=acc_of[j][:],
                         lhsT=codes[:, half, cols].bitcast(FP8X4),
@@ -190,7 +198,10 @@ def tile_gaussiankernel_kernel(tc, x, grid, spline_weight_words, spline_weight_s
         def store_chunk(chunk):
             for j in range(CHUNK_TILES):
                 res = res_pool.tile([P, OUT], F32)
-                nc.vector.tensor_copy(out=res[:], in_=acc_of[j][:])
+                if j % 2 == 0:
+                    nc.vector.tensor_copy(out=res[:], in_=acc_of[j][:])
+                else:
+                    nc.scalar.copy(out=res[:], in_=acc_of[j][:])
                 nc.sync.dma_start(out=out_rows[:, chunk * CHUNK_TILES + j, :], in_=res[:])
 
         def valid(s):

@@ -10,6 +10,7 @@ U32 = mybir.dt.uint32
 U8 = mybir.dt.uint8
 FP8X4 = mybir.dt.float8_e4m3fn_x4
 ACT = mybir.ActivationFunctionType
+ALU = mybir.AluOpType
 
 P = 128
 PACK = 4
@@ -25,7 +26,7 @@ PAIR = 2
 STEPS_PER_CHUNK = PASSES // PAIR
 STEPS = (ROW_TILES // CHUNK_TILES) * STEPS_PER_CHUNK
 
-SCALAR_COLS = 128
+SCALAR_COLS = 64
 VECTOR_COLS = CHUNK - SCALAR_COLS
 
 FLOPS = 2 * BATCH * FEATURES * GRID * OUT
@@ -38,14 +39,14 @@ def tile_gaussiankernel_kernel(tc, x, grid, spline_weight_words, spline_weight_s
 
     with ExitStack() as ctx:
         keep = ctx.enter_context(tc.tile_pool(name="keep", bufs=1))
-        xt_pool = ctx.enter_context(tc.tile_pool(name="xt", bufs=3))
+        xt_pool = ctx.enter_context(tc.tile_pool(name="xt", bufs=2))
         xr_pool = ctx.enter_context(tc.tile_pool(name="xr", bufs=2))
-        sq_pool = ctx.enter_context(tc.tile_pool(name="sq", bufs=3))
+        sq_pool = ctx.enter_context(tc.tile_pool(name="sq", bufs=4))
         basis_pool = ctx.enter_context(tc.tile_pool(name="basis", bufs=2))
         mx_pool = ctx.enter_context(tc.tile_pool(name="mx", bufs=2))
         res_pool = ctx.enter_context(tc.tile_pool(name="res", bufs=4))
-        xt_psum = ctx.enter_context(tc.psum_pool(name="xt_psum", bufs=2))
-        xr_psum = ctx.enter_context(tc.psum_pool(name="xr_psum", bufs=2))
+        xt_psum = ctx.enter_context(tc.psum_pool(name="xt_psum", bufs=1))
+        xr_psum = ctx.enter_context(tc.psum_pool(name="xr_psum", bufs=3))
         acc_psum = ctx.enter_context(tc.psum_pool(name="acc_psum", bufs=1))
         ctx.enter_context(tc.manual_schedule())
 
@@ -140,15 +141,31 @@ def tile_gaussiankernel_kernel(tc, x, grid, spline_weight_words, spline_weight_s
             sq_of[s] = sq
             xr_of[s] = xr
 
-        def vector_squares(s):
+        def gpsimd_differences(s):
             sq = sq_of[s]
             xr = xr_of[s]
             for t in range(PACK):
-                nc.vector.tensor_scalar_add(
-                    out=sq[:, :, t, SCALAR_COLS:CHUNK], in0=xr[:], scalar1=neg_grid[:, t : t + 1]
+                nc.gpsimd.tensor_scalar(
+                    out=sq[:, :, t, SCALAR_COLS:CHUNK],
+                    in0=xr[:],
+                    scalar1=1.0,
+                    scalar2=neg_grid[:, t : t + 1],
+                    op0=ALU.mult,
+                    op1=ALU.add,
                 )
-            rest = sq[:, :, :, SCALAR_COLS:CHUNK]
-            nc.vector.tensor_mul(out=rest, in0=rest, in1=rest)
+
+        def vector_squares(s):
+            sq = sq_of[s]
+            xr_ps = xr_ps_of[s]
+            for t in range(PACK):
+                nc.vector.scalar_tensor_tensor(
+                    out=sq[:, :, t, SCALAR_COLS:CHUNK],
+                    in0=xr_ps[:, :, SCALAR_COLS:CHUNK],
+                    scalar=neg_grid[:, t : t + 1],
+                    in1=sq[:, :, t, SCALAR_COLS:CHUNK],
+                    op0=ALU.add,
+                    op1=ALU.mult,
+                )
 
         def exponentials(s):
             sq = sq_of[s]
@@ -217,7 +234,9 @@ def tile_gaussiankernel_kernel(tc, x, grid, spline_weight_words, spline_weight_s
             if valid(k + 1):
                 vector_squares(k + 1)
             if valid(k + 2):
-                scalar_squares(k + 2)
+                gpsimd_differences(k + 2)
+            if valid(k + 3):
+                scalar_squares(k + 3)
             if valid(k + 4):
                 copy_transposed(k + 4)
             if k > 0 and k % STEPS_PER_CHUNK == 0:

@@ -26,8 +26,10 @@ PAIR = 2
 STEPS_PER_CHUNK = PASSES // PAIR
 STEPS = (ROW_TILES // CHUNK_TILES) * STEPS_PER_CHUNK
 
-SCALAR_COLS = 64
-VECTOR_COLS = CHUNK - SCALAR_COLS
+SCALAR_COLS = 128
+RUN = 4
+STEP_COLS = PAIR * CHUNK
+VECTOR_COLS = STEP_COLS - SCALAR_COLS
 
 FLOPS = 2 * BATCH * FEATURES * GRID * OUT
 
@@ -127,17 +129,18 @@ def tile_gaussiankernel_kernel(tc, x, grid, spline_weight_words, spline_weight_s
 
         def scalar_squares(s):
             xr_ps = xr_ps_of[s]
-            sq = sq_pool.tile([P, PAIR, PACK, CHUNK], F32)
+            sq = sq_pool.tile([P, STEP_COLS // RUN, PACK, RUN], F32)
+            flat = xr_ps[:].rearrange("p h b -> p (h b)")
             for t in range(PACK):
                 nc.scalar.activation(
-                    out=sq[:, :, t, 0:SCALAR_COLS],
-                    in_=xr_ps[:, :, 0:SCALAR_COLS],
+                    out=sq[:, 0 : SCALAR_COLS // RUN, t, :],
+                    in_=flat[:, 0:SCALAR_COLS].rearrange("p (c i) -> p c i", i=RUN),
                     func=ACT.Square,
                     bias=neg_grid[:, t : t + 1],
                     scale=1.0,
                 )
-            xr = xr_pool.tile([P, PAIR, VECTOR_COLS], BF16)
-            nc.scalar.copy(out=xr[:], in_=xr_ps[:, :, SCALAR_COLS:CHUNK])
+            xr = xr_pool.tile([P, VECTOR_COLS], BF16)
+            nc.scalar.copy(out=xr[:], in_=flat[:, SCALAR_COLS:STEP_COLS])
             sq_of[s] = sq
             xr_of[s] = xr
 
@@ -146,8 +149,8 @@ def tile_gaussiankernel_kernel(tc, x, grid, spline_weight_words, spline_weight_s
             xr = xr_of[s]
             for t in range(PACK):
                 nc.gpsimd.tensor_scalar(
-                    out=sq[:, :, t, SCALAR_COLS:CHUNK],
-                    in0=xr[:],
+                    out=sq[:, SCALAR_COLS // RUN : STEP_COLS // RUN, t, :],
+                    in0=xr[:].rearrange("p (c i) -> p c i", i=RUN),
                     scalar1=1.0,
                     scalar2=neg_grid[:, t : t + 1],
                     op0=ALU.mult,
@@ -157,12 +160,12 @@ def tile_gaussiankernel_kernel(tc, x, grid, spline_weight_words, spline_weight_s
         def vector_squares(s):
             sq = sq_of[s]
             xr_ps = xr_ps_of[s]
-            for t in range(PACK):
+            for t in (PACK - 1,) + tuple(range(PACK - 1)):
                 nc.vector.scalar_tensor_tensor(
-                    out=sq[:, :, t, SCALAR_COLS:CHUNK],
-                    in0=xr_ps[:, :, SCALAR_COLS:CHUNK],
+                    out=sq[:, SCALAR_COLS // RUN : STEP_COLS // RUN, t, :],
+                    in0=xr_ps[:].rearrange("p h b -> p (h b)")[:, SCALAR_COLS:STEP_COLS].rearrange("p (c i) -> p c i", i=RUN),
                     scalar=neg_grid[:, t : t + 1],
-                    in1=sq[:, :, t, SCALAR_COLS:CHUNK],
+                    in1=sq[:, SCALAR_COLS // RUN : STEP_COLS // RUN, t, :],
                     op0=ALU.add,
                     op1=ALU.mult,
                 )
@@ -172,8 +175,8 @@ def tile_gaussiankernel_kernel(tc, x, grid, spline_weight_words, spline_weight_s
             basis = basis_pool.tile([P, PAIR, CHUNK, PACK], BF16, align_bytes=64)
             for half in range(PAIR):
                 nc.scalar.activation(
-                    out=basis[:, half, :, :].rearrange("p (c i) t -> p c t i", i=4),
-                    in_=sq[:, half, :, :].rearrange("p t (c i) -> p c t i", i=4),
+                    out=basis[:, half, :, :].rearrange("p (c i) t -> p c t i", i=RUN),
+                    in_=sq[:, half * (CHUNK // RUN) : (half + 1) * (CHUNK // RUN), :, :],
                     func=ACT.Exp,
                     scale=-INV_H2,
                 )

@@ -24,14 +24,20 @@ CHUNK_TILES = 4
 CHUNK = CHUNK_TILES * P
 PAIR = 2
 STEPS_PER_CHUNK = PASSES // PAIR
-STEPS = (ROW_TILES // CHUNK_TILES) * STEPS_PER_CHUNK
-
-SCALAR_COLS = 128
-RUN = 4
+CHUNKS = ROW_TILES // CHUNK_TILES
+STEPS = CHUNKS * STEPS_PER_CHUNK
 STEP_COLS = PAIR * CHUNK
-VECTOR_COLS = STEP_COLS - SCALAR_COLS
+RUN = 4
 
 FLOPS = 2 * BATCH * FEATURES * GRID * OUT
+
+
+def scalar_planes(s):
+    return tuple(range(PACK)) if s == 0 else (PACK - 1,)
+
+
+def vector_planes(s):
+    return tuple([t for t in range(PACK) if t not in scalar_planes(s)])
 
 
 def tile_gaussiankernel_kernel(tc, x, grid, spline_weight_words, spline_weight_scales, out):
@@ -44,21 +50,13 @@ def tile_gaussiankernel_kernel(tc, x, grid, spline_weight_words, spline_weight_s
         xt_pool = ctx.enter_context(tc.tile_pool(name="xt", bufs=2))
         xr_pool = ctx.enter_context(tc.tile_pool(name="xr", bufs=2))
         sq_pool = ctx.enter_context(tc.tile_pool(name="sq", bufs=4))
-        basis_pool = ctx.enter_context(tc.tile_pool(name="basis", bufs=2))
-        mx_pool = ctx.enter_context(tc.tile_pool(name="mx", bufs=2))
+        basis_pool = ctx.enter_context(tc.tile_pool(name="basis", bufs=3))
+        mx_pool = ctx.enter_context(tc.tile_pool(name="mx", bufs=3))
         res_pool = ctx.enter_context(tc.tile_pool(name="res", bufs=4))
         xt_psum = ctx.enter_context(tc.psum_pool(name="xt_psum", bufs=1))
         xr_psum = ctx.enter_context(tc.psum_pool(name="xr_psum", bufs=3))
         acc_psum = ctx.enter_context(tc.psum_pool(name="acc_psum", bufs=1))
         ctx.enter_context(tc.manual_schedule())
-
-        w_scales = keep.tile([P, PASSES, OUT], U8, align_bytes=64)
-        nc.vector.memset(w_scales[:].rearrange("p g n -> p (g n)").bitcast(I32), 0)
-
-        grid_bf = keep.tile([P, PACK], BF16)
-        with nc.allow_non_contiguous_dma(reason="eight bytes of the grid to each partition"):
-            nc.sync.dma_start(out=grid_bf[0:P:2, :], in_=grid[0:PACK].partition_broadcast(P // 2))
-            nc.sync.dma_start(out=grid_bf[1:P:2, :], in_=grid[PACK:GRID].partition_broadcast(P // 2))
 
         x_sb = keep.tile([P, ROW_TILES, FEATURES], BF16)
 
@@ -68,7 +66,20 @@ def tile_gaussiankernel_kernel(tc, x, grid, spline_weight_words, spline_weight_s
             cols = slice(part * P, (part + 1) * P)
             nc.sync.dma_start(out=x_sb[:, rows, cols], in_=x_rows[:, rows, cols])
 
-        for s in range(STEPS_PER_CHUNK):
+        load_x(0)
+
+        warm = keep.tile([P, 2], F32)
+        nc.vector.memset(warm[:], 0.0)
+        nc.scalar.activation(out=warm[:, 1:2], in_=warm[:, 0:1], func=ACT.Exp)
+
+        w_scales = keep.tile([P, PASSES, OUT], U8, align_bytes=64)
+        nc.vector.memset(w_scales[:].rearrange("p g n -> p (g n)").bitcast(I32), 0)
+
+        grid_bf = keep.tile([P, PACK], BF16)
+        with nc.allow_non_contiguous_dma(reason="eight bytes of the grid to each partition"):
+            nc.sync.dma_start(out=grid_bf[0:P:2, :], in_=grid[0:PACK].partition_broadcast(P // 2))
+            nc.sync.dma_start(out=grid_bf[1:P:2, :], in_=grid[PACK:GRID].partition_broadcast(P // 2))
+        for s in range(1, STEPS_PER_CHUNK):
             load_x(s)
 
         for quad in range(4):
@@ -77,11 +88,15 @@ def tile_gaussiankernel_kernel(tc, x, grid, spline_weight_words, spline_weight_s
                 in_=spline_weight_scales[:, 4 * quad : 4 * quad + 4, :].rearrange("g r n -> r g n").bitcast(I32),
             )
         w_words = keep.tile([P, PASSES, OUT], U32, align_bytes=64)
-        for g in range(PASSES):
+
+        def load_weight(g):
             nc.sync.dma_start(
                 out=w_words[:, g, :].bitcast(I32),
                 in_=spline_weight_words[g].rearrange("p n t -> p (n t)").bitcast(I32),
             )
+
+        for g in range(PASSES):
+            load_weight(g)
         for s in range(STEPS_PER_CHUNK, STEPS):
             load_x(s)
 
@@ -111,7 +126,7 @@ def tile_gaussiankernel_kernel(tc, x, grid, spline_weight_words, spline_weight_s
 
         def copy_transposed(s):
             xt = xt_pool.tile([P, CHUNK], BF16)
-            nc.scalar.copy(out=xt[:], in_=xt_ps_of[s][:])
+            nc.vector.tensor_copy(out=xt[:], in_=xt_ps_of[s][:])
             xt_of[s] = xt
 
         def spread_features(s):
@@ -127,30 +142,26 @@ def tile_gaussiankernel_kernel(tc, x, grid, spline_weight_words, spline_weight_s
                 )
             xr_ps_of[s] = xr_ps
 
-        def scalar_squares(s):
-            xr_ps = xr_ps_of[s]
-            sq = sq_pool.tile([P, STEP_COLS // RUN, PACK, RUN], F32)
-            flat = xr_ps[:].rearrange("p h b -> p (h b)")
-            for t in range(PACK):
-                nc.scalar.activation(
-                    out=sq[:, 0 : SCALAR_COLS // RUN, t, :],
-                    in_=flat[:, 0:SCALAR_COLS].rearrange("p (c i) -> p c i", i=RUN),
-                    func=ACT.Square,
-                    bias=neg_grid[:, t : t + 1],
-                    scale=1.0,
-                )
-            xr = xr_pool.tile([P, VECTOR_COLS], BF16)
-            nc.scalar.copy(out=xr[:], in_=flat[:, SCALAR_COLS:STEP_COLS])
-            sq_of[s] = sq
-            xr_of[s] = xr
+        def copy_spread(s):
+            if vector_planes(s):
+                xr = xr_pool.tile([P, PAIR, CHUNK], BF16)
+                nc.vector.tensor_copy(out=xr[:], in_=xr_ps_of[s][:])
+                xr_of[s] = xr
+
+        def squares_tile(s):
+            if s not in sq_of:
+                sq_of[s] = sq_pool.tile([P, STEP_COLS // RUN, PACK, RUN], F32, name="sq")
+            return sq_of[s]
+
+        def runs(ap):
+            return ap.rearrange("p h b -> p (h b)").rearrange("p (c i) -> p c i", i=RUN)
 
         def gpsimd_differences(s):
-            sq = sq_of[s]
-            xr = xr_of[s]
-            for t in range(PACK):
+            sq = squares_tile(s)
+            for t in vector_planes(s):
                 nc.gpsimd.tensor_scalar(
-                    out=sq[:, SCALAR_COLS // RUN : STEP_COLS // RUN, t, :],
-                    in0=xr[:].rearrange("p (c i) -> p c i", i=RUN),
+                    out=sq[:, :, t, :],
+                    in0=runs(xr_of[s][:]),
                     scalar1=1.0,
                     scalar2=neg_grid[:, t : t + 1],
                     op0=ALU.mult,
@@ -158,16 +169,26 @@ def tile_gaussiankernel_kernel(tc, x, grid, spline_weight_words, spline_weight_s
                 )
 
         def vector_squares(s):
-            sq = sq_of[s]
-            xr_ps = xr_ps_of[s]
-            for t in (PACK - 1,) + tuple(range(PACK - 1)):
+            sq = squares_tile(s)
+            for t in reversed(vector_planes(s)):
                 nc.vector.scalar_tensor_tensor(
-                    out=sq[:, SCALAR_COLS // RUN : STEP_COLS // RUN, t, :],
-                    in0=xr_ps[:].rearrange("p h b -> p (h b)")[:, SCALAR_COLS:STEP_COLS].rearrange("p (c i) -> p c i", i=RUN),
+                    out=sq[:, :, t, :],
+                    in0=runs(xr_ps_of[s][:]),
                     scalar=neg_grid[:, t : t + 1],
-                    in1=sq[:, SCALAR_COLS // RUN : STEP_COLS // RUN, t, :],
+                    in1=sq[:, :, t, :],
                     op0=ALU.add,
                     op1=ALU.mult,
+                )
+
+        def scalar_squares(s):
+            sq = squares_tile(s)
+            for t in scalar_planes(s):
+                nc.scalar.activation(
+                    out=sq[:, :, t, :],
+                    in_=runs(xr_ps_of[s][:]),
+                    func=ACT.Square,
+                    bias=neg_grid[:, t : t + 1],
+                    scale=1.0,
                 )
 
         def exponentials(s):
@@ -218,32 +239,33 @@ def tile_gaussiankernel_kernel(tc, x, grid, spline_weight_words, spline_weight_s
         def store_chunk(chunk):
             for j in range(CHUNK_TILES):
                 res = res_pool.tile([P, OUT], F32)
-                if j % 2 == 0:
-                    nc.vector.tensor_copy(out=res[:], in_=acc_of[j][:])
-                else:
+                if chunk == CHUNKS - 1 and j % 2 == 1:
                     nc.scalar.copy(out=res[:], in_=acc_of[j][:])
+                else:
+                    nc.vector.tensor_copy(out=res[:], in_=acc_of[j][:])
                 nc.sync.dma_start(out=out_rows[:, chunk * CHUNK_TILES + j, :], in_=res[:])
 
         def valid(s):
             return 0 <= s < STEPS
 
         for k in range(-4, STEPS + 1):
-            if valid(k + 4):
-                transpose_features(k + 4)
             if valid(k + 3):
                 spread_features(k + 3)
-            if valid(k):
-                exponentials(k)
-            if valid(k + 1):
-                vector_squares(k + 1)
+            if valid(k + 4):
+                transpose_features(k + 4)
+            if valid(k - 1):
+                quantise(k - 1)
+                multiply(k - 1)
             if valid(k + 2):
                 gpsimd_differences(k + 2)
+            if valid(k + 1):
+                vector_squares(k + 1)
+                scalar_squares(k + 1)
+            if valid(k):
+                exponentials(k)
+            if valid(k - 1) and k % STEPS_PER_CHUNK == 0:
+                store_chunk(k // STEPS_PER_CHUNK - 1)
             if valid(k + 3):
-                scalar_squares(k + 3)
+                copy_spread(k + 3)
             if valid(k + 4):
                 copy_transposed(k + 4)
-            if k > 0 and k % STEPS_PER_CHUNK == 0:
-                store_chunk(k // STEPS_PER_CHUNK - 1)
-            if valid(k):
-                quantise(k)
-                multiply(k)

@@ -239,7 +239,7 @@ def tile_gaussiankernel_kernel(tc, x, grid, spline_weight_words, spline_weight_s
         def store_chunk(chunk):
             for j in range(CHUNK_TILES):
                 res = res_pool.tile([P, OUT], F32)
-                if chunk == CHUNKS - 1 and j % 2 == 1:
+                if j % 2 == 1:
                     nc.scalar.copy(out=res[:], in_=acc_of[j][:])
                 else:
                     nc.vector.tensor_copy(out=res[:], in_=acc_of[j][:])
@@ -253,19 +253,19 @@ def tile_gaussiankernel_kernel(tc, x, grid, spline_weight_words, spline_weight_s
                 spread_features(k + 3)
             if valid(k + 4):
                 transpose_features(k + 4)
-            if valid(k - 1):
-                quantise(k - 1)
-                multiply(k - 1)
             if valid(k + 2):
                 gpsimd_differences(k + 2)
+                scalar_squares(k + 2)
             if valid(k + 1):
                 vector_squares(k + 1)
-                scalar_squares(k + 1)
-            if valid(k):
-                exponentials(k)
-            if valid(k - 1) and k % STEPS_PER_CHUNK == 0:
-                store_chunk(k // STEPS_PER_CHUNK - 1)
             if valid(k + 3):
                 copy_spread(k + 3)
             if valid(k + 4):
                 copy_transposed(k + 4)
+            if valid(k):
+                exponentials(k)
+            if valid(k - 1):
+                quantise(k - 1)
+                multiply(k - 1)
+            if valid(k - 1) and k % STEPS_PER_CHUNK == 0:
+                store_chunk(k // STEPS_PER_CHUNK - 1)

@@ -40,6 +40,12 @@ def vector_planes(s):
     return tuple([t for t in range(PACK) if t not in scalar_planes(s)])
 
 
+def pieces(s):
+    if s == STEPS - 1:
+        return [(0, 0, CHUNK_TILES)] + [(1, j, 1) for j in range(CHUNK_TILES)]
+    return [(half, 0, CHUNK_TILES) for half in range(PAIR)]
+
+
 def tile_gaussiankernel_kernel(tc, x, grid, spline_weight_words, spline_weight_scales, out):
     nc = tc.nc
     x_rows = x.rearrange("(p r) i -> p r i", r=ROW_TILES)
@@ -49,6 +55,7 @@ def tile_gaussiankernel_kernel(tc, x, grid, spline_weight_words, spline_weight_s
         keep = ctx.enter_context(tc.tile_pool(name="keep", bufs=1))
         xt_pool = ctx.enter_context(tc.tile_pool(name="xt", bufs=2))
         xr_pool = ctx.enter_context(tc.tile_pool(name="xr", bufs=2))
+        diff_pool = ctx.enter_context(tc.tile_pool(name="diff", bufs=3))
         sq_pool = ctx.enter_context(tc.tile_pool(name="sq", bufs=4))
         basis_pool = ctx.enter_context(tc.tile_pool(name="basis", bufs=3))
         mx_pool = ctx.enter_context(tc.tile_pool(name="mx", bufs=3))
@@ -111,7 +118,8 @@ def tile_gaussiankernel_kernel(tc, x, grid, spline_weight_words, spline_weight_s
         neg_grid = keep.tile([P, PACK], F32)
         nc.vector.tensor_scalar_mul(out=neg_grid[:], in0=grid_bf[:], scalar1=-1.0)
 
-        xt_ps_of, xt_of, xr_ps_of, xr_of, sq_of, basis_of, codes_of, scales_of, acc_of = {}, {}, {}, {}, {}, {}, {}, {}, {}
+        xt_ps_of, xt_of, xr_ps_of, xr_of, diff_of, sq_of, basis_of = {}, {}, {}, {}, {}, {}, {}
+        codes_of, scales_of, acc_of = {}, {}, {}
 
         def transpose_features(s):
             chunk, part = divmod(s, STEPS_PER_CHUNK)
@@ -157,25 +165,27 @@ def tile_gaussiankernel_kernel(tc, x, grid, spline_weight_words, spline_weight_s
             return ap.rearrange("p h b -> p (h b)").rearrange("p (c i) -> p c i", i=RUN)
 
         def gpsimd_differences(s):
-            sq = squares_tile(s)
-            for t in vector_planes(s):
-                nc.gpsimd.tensor_scalar(
-                    out=sq[:, :, t, :],
-                    in0=runs(xr_of[s][:]),
-                    scalar1=1.0,
-                    scalar2=neg_grid[:, t : t + 1],
-                    op0=ALU.mult,
-                    op1=ALU.add,
-                )
+            if vector_planes(s):
+                diff = diff_pool.tile([P, PACK - 1, STEP_COLS], F32)
+                for t in vector_planes(s):
+                    nc.gpsimd.tensor_scalar(
+                        out=diff[:, t, :],
+                        in0=xr_of[s][:].rearrange("p h b -> p (h b)"),
+                        scalar1=1.0,
+                        scalar2=neg_grid[:, t : t + 1],
+                        op0=ALU.mult,
+                        op1=ALU.add,
+                    )
+                diff_of[s] = diff
 
         def vector_squares(s):
             sq = squares_tile(s)
-            for t in reversed(vector_planes(s)):
+            for t in vector_planes(s):
                 nc.vector.scalar_tensor_tensor(
                     out=sq[:, :, t, :],
                     in0=runs(xr_ps_of[s][:]),
                     scalar=neg_grid[:, t : t + 1],
-                    in1=sq[:, :, t, :],
+                    in1=diff_of[s][:, t, :].rearrange("p (c i) -> p c i", i=RUN),
                     op0=ALU.add,
                     op1=ALU.mult,
                 )
@@ -194,10 +204,11 @@ def tile_gaussiankernel_kernel(tc, x, grid, spline_weight_words, spline_weight_s
         def exponentials(s):
             sq = sq_of[s]
             basis = basis_pool.tile([P, PAIR, CHUNK, PACK], BF16, align_bytes=64)
-            for half in range(PAIR):
+            for half, j0, n in pieces(s):
+                first = (half * CHUNK + j0 * P) // RUN
                 nc.scalar.activation(
-                    out=basis[:, half, :, :].rearrange("p (c i) t -> p c t i", i=RUN),
-                    in_=sq[:, half * (CHUNK // RUN) : (half + 1) * (CHUNK // RUN), :, :],
+                    out=basis[:, half, j0 * P : (j0 + n) * P, :].rearrange("p (c i) t -> p c t i", i=RUN),
+                    in_=sq[:, first : first + n * P // RUN, :, :],
                     func=ACT.Exp,
                     scale=-INV_H2,
                 )
@@ -207,11 +218,12 @@ def tile_gaussiankernel_kernel(tc, x, grid, spline_weight_words, spline_weight_s
             basis = basis_of[s]
             codes = mx_pool.tile([P, PAIR, CHUNK], U32, align_bytes=64)
             scales = mx_pool.tile([P, PAIR, CHUNK], U8, align_bytes=64)
-            for half in range(PAIR):
+            for half, j0, n in pieces(s):
+                cols = slice(j0 * P, (j0 + n) * P)
                 nc.vector.quantize_mx(
-                    out=codes[:, half, :].bitcast(FP8X4),
-                    scales=scales[:, half, :],
-                    in_=basis[:, half, :, :].rearrange("p b t -> p (b t)"),
+                    out=codes[:, half, cols].bitcast(FP8X4),
+                    scales=scales[:, half, cols],
+                    in_=basis[:, half, cols, :].rearrange("p b t -> p (b t)"),
                 )
             codes_of[s] = codes
             scales_of[s] = scales

@@ -260,11 +260,13 @@ def tile_gaussiankernel_kernel(tc, x, grid, spline_weight_words, spline_weight_s
         def valid(s):
             return 0 <= s < STEPS
 
-        for k in range(-4, STEPS + 1):
+        for k in range(-4, STEPS + 2):
             if valid(k + 3):
                 spread_features(k + 3)
             if valid(k + 4):
                 transpose_features(k + 4)
+            if valid(k - 2):
+                multiply(k - 2)
             if valid(k + 2):
                 gpsimd_differences(k + 2)
                 scalar_squares(k + 2)
@@ -278,6 +280,5 @@ def tile_gaussiankernel_kernel(tc, x, grid, spline_weight_words, spline_weight_s
                 exponentials(k)
             if valid(k - 1):
                 quantise(k - 1)
-                multiply(k - 1)
-            if valid(k - 1) and k % STEPS_PER_CHUNK == 0:
-                store_chunk(k // STEPS_PER_CHUNK - 1)
+            if valid(k - 2) and (k - 1) % STEPS_PER_CHUNK == 0:
+                store_chunk((k - 1) // STEPS_PER_CHUNK - 1)

@@ -54,7 +54,6 @@ def tile_gaussiankernel_kernel(tc, x, grid, spline_weight_words, spline_weight_s
     with ExitStack() as ctx:
         keep = ctx.enter_context(tc.tile_pool(name="keep", bufs=1))
         xt_pool = ctx.enter_context(tc.tile_pool(name="xt", bufs=2))
-        xr_pool = ctx.enter_context(tc.tile_pool(name="xr", bufs=2))
         diff_pool = ctx.enter_context(tc.tile_pool(name="diff", bufs=3))
         sq_pool = ctx.enter_context(tc.tile_pool(name="sq", bufs=4))
         basis_pool = ctx.enter_context(tc.tile_pool(name="basis", bufs=3))
@@ -117,8 +116,19 @@ def tile_gaussiankernel_kernel(tc, x, grid, spline_weight_words, spline_weight_s
             )
         neg_grid = keep.tile([P, PACK], F32)
         nc.vector.tensor_scalar_mul(out=neg_grid[:], in0=grid_bf[:], scalar1=-1.0)
+        last = neg_grid[:, PACK - 1 : PACK]
+        step_to_last = keep.tile([P, PACK - 1], F32)
+        slope = keep.tile([P, PACK - 1], F32)
+        constant = keep.tile([P, PACK - 1], F32)
+        nc.vector.tensor_scalar(
+            out=step_to_last[:], in0=neg_grid[:, 0 : PACK - 1], scalar1=last, scalar2=1.0, op0=ALU.subtract, op1=ALU.mult
+        )
+        nc.vector.tensor_scalar_mul(out=slope[:], in0=step_to_last[:], scalar1=2.0)
+        nc.vector.scalar_tensor_tensor(
+            out=constant[:], in0=neg_grid[:, 0 : PACK - 1], scalar=last, in1=step_to_last[:], op0=ALU.add, op1=ALU.mult
+        )
 
-        xt_ps_of, xt_of, xr_ps_of, xr_of, diff_of, sq_of, basis_of = {}, {}, {}, {}, {}, {}, {}
+        xt_ps_of, xt_of, xr_ps_of, diff_of, sq_of, basis_of = {}, {}, {}, {}, {}, {}
         codes_of, scales_of, acc_of = {}, {}, {}
 
         def transpose_features(s):
@@ -150,12 +160,6 @@ def tile_gaussiankernel_kernel(tc, x, grid, spline_weight_words, spline_weight_s
                 )
             xr_ps_of[s] = xr_ps
 
-        def copy_spread(s):
-            if vector_planes(s):
-                xr = xr_pool.tile([P, PAIR, CHUNK], BF16)
-                nc.vector.tensor_copy(out=xr[:], in_=xr_ps_of[s][:])
-                xr_of[s] = xr
-
         def squares_tile(s):
             if s not in sq_of:
                 sq_of[s] = sq_pool.tile([P, STEP_COLS // RUN, PACK, RUN], F32, name="sq")
@@ -164,15 +168,15 @@ def tile_gaussiankernel_kernel(tc, x, grid, spline_weight_words, spline_weight_s
         def runs(ap):
             return ap.rearrange("p h b -> p (h b)").rearrange("p (c i) -> p c i", i=RUN)
 
-        def gpsimd_differences(s):
+        def gpsimd_constants(s):
             if vector_planes(s):
                 diff = diff_pool.tile([P, PACK - 1, STEP_COLS], F32)
                 for t in vector_planes(s):
                     nc.gpsimd.tensor_scalar(
-                        out=diff[:, t, :],
-                        in0=xr_of[s][:].rearrange("p h b -> p (h b)"),
+                        out=diff[:, t, :].rearrange("p (c i) -> p c i", i=RUN),
+                        in0=sq_of[s][:, :, PACK - 1, :],
                         scalar1=1.0,
-                        scalar2=neg_grid[:, t : t + 1],
+                        scalar2=constant[:, t : t + 1],
                         op0=ALU.mult,
                         op1=ALU.add,
                     )
@@ -184,10 +188,10 @@ def tile_gaussiankernel_kernel(tc, x, grid, spline_weight_words, spline_weight_s
                 nc.vector.scalar_tensor_tensor(
                     out=sq[:, :, t, :],
                     in0=runs(xr_ps_of[s][:]),
-                    scalar=neg_grid[:, t : t + 1],
+                    scalar=slope[:, t : t + 1],
                     in1=diff_of[s][:, t, :].rearrange("p (c i) -> p c i", i=RUN),
-                    op0=ALU.add,
-                    op1=ALU.mult,
+                    op0=ALU.mult,
+                    op1=ALU.add,
                 )
 
         def scalar_squares(s):
@@ -251,7 +255,7 @@ def tile_gaussiankernel_kernel(tc, x, grid, spline_weight_words, spline_weight_s
         def store_chunk(chunk):
             for j in range(CHUNK_TILES):
                 res = res_pool.tile([P, OUT], F32)
-                if j % 2 == 1:
+                if chunk == CHUNKS - 1 and j % 2 == 1:
                     nc.scalar.copy(out=res[:], in_=acc_of[j][:])
                 else:
                     nc.vector.tensor_copy(out=res[:], in_=acc_of[j][:])
@@ -268,12 +272,10 @@ def tile_gaussiankernel_kernel(tc, x, grid, spline_weight_words, spline_weight_s
             if valid(k - 2):
                 multiply(k - 2)
             if valid(k + 2):
-                gpsimd_differences(k + 2)
                 scalar_squares(k + 2)
+                gpsimd_constants(k + 2)
             if valid(k + 1):
                 vector_squares(k + 1)
-            if valid(k + 3):
-                copy_spread(k + 3)
             if valid(k + 4):
                 copy_transposed(k + 4)
             if valid(k):

@@ -33,7 +33,7 @@ FLOPS = 2 * BATCH * FEATURES * GRID * OUT
 
 
 def scalar_planes(s):
-    return tuple(range(PACK)) if s == 0 else (PACK - 1,)
+    return (PACK - 1,)
 
 
 def vector_planes(s):
@@ -128,7 +128,7 @@ def tile_gaussiankernel_kernel(tc, x, grid, spline_weight_words, spline_weight_s
             out=constant[:], in0=neg_grid[:, 0 : PACK - 1], scalar=last, in1=step_to_last[:], op0=ALU.add, op1=ALU.mult
         )
 
-        xt_ps_of, xt_of, xr_ps_of, diff_of, sq_of, basis_of = {}, {}, {}, {}, {}, {}
+        xt_ps_of, xt_of, xr_ps_of, halves_of, diff_of, sq_of, basis_of = {}, {}, {}, {}, {}, {}, {}
         codes_of, scales_of, acc_of = {}, {}, {}
 
         def transpose_features(s):
@@ -149,66 +149,85 @@ def tile_gaussiankernel_kernel(tc, x, grid, spline_weight_words, spline_weight_s
 
         def spread_features(s):
             xr_ps = xr_psum.tile([P, PAIR, CHUNK], BF16)
+            halves = [xr_ps[:, half, :] for half in range(PAIR)]
+            if s == 0:
+                second = acc_psum.tile([P, CHUNK], BF16, name="first_x", tag="acc_%d" % (CHUNK_TILES - 1))
+                halves[1] = second[:]
             xt = xt_of[s]
             for half in range(PAIR):
                 nc.tensor.matmul(
-                    out=xr_ps[:, half, :],
+                    out=halves[half],
                     lhsT=spread[:, half, :, :].rearrange("p i c -> p (i c)"),
                     rhs=xt[:],
                     start=True,
                     stop=True,
                 )
             xr_ps_of[s] = xr_ps
+            halves_of[s] = halves
+
+        def spread_x(s, half):
+            if half is None:
+                return xr_ps_of[s][:].rearrange("p h b -> p (h b)").rearrange("p (c i) -> p c i", i=RUN)
+            return halves_of[s][half].rearrange("p (c i) -> p c i", i=RUN)
+
+        def run_range(half):
+            per_half = CHUNK // RUN
+            return slice(0, PAIR * per_half) if half is None else slice(half * per_half, (half + 1) * per_half)
 
         def squares_tile(s):
             if s not in sq_of:
                 sq_of[s] = sq_pool.tile([P, STEP_COLS // RUN, PACK, RUN], F32, name="sq")
             return sq_of[s]
 
-        def runs(ap):
-            return ap.rearrange("p h b -> p (h b)").rearrange("p (c i) -> p c i", i=RUN)
+        def add_constant(engine, s, t, half=None):
+            if (s, t) not in diff_of:
+                diff_of[s, t] = diff_pool.tile([P, STEP_COLS // RUN, RUN], F32, name="diff_%d" % t, tag="diff_%d" % t)
+            engine.tensor_scalar(
+                out=diff_of[s, t][:, run_range(half), :],
+                in0=sq_of[s][:, run_range(half), PACK - 1, :],
+                scalar1=1.0,
+                scalar2=constant[:, t : t + 1],
+                op0=ALU.mult,
+                op1=ALU.add,
+            )
 
         def gpsimd_constants(s):
-            if vector_planes(s):
-                diff = diff_pool.tile([P, PACK - 1, STEP_COLS], F32)
-                for t in vector_planes(s):
-                    nc.gpsimd.tensor_scalar(
-                        out=diff[:, t, :].rearrange("p (c i) -> p c i", i=RUN),
-                        in0=sq_of[s][:, :, PACK - 1, :],
-                        scalar1=1.0,
-                        scalar2=constant[:, t : t + 1],
-                        op0=ALU.mult,
-                        op1=ALU.add,
-                    )
-                diff_of[s] = diff
+            for t in vector_planes(s):
+                add_constant(nc.gpsimd, s, t)
+
+        def add_slope(s, t, half=None):
+            nc.vector.scalar_tensor_tensor(
+                out=squares_tile(s)[:, run_range(half), t, :],
+                in0=spread_x(s, half),
+                scalar=slope[:, t : t + 1],
+                in1=diff_of[s, t][:, run_range(half), :],
+                op0=ALU.mult,
+                op1=ALU.add,
+            )
 
         def vector_squares(s):
-            sq = squares_tile(s)
             for t in vector_planes(s):
-                nc.vector.scalar_tensor_tensor(
-                    out=sq[:, :, t, :],
-                    in0=runs(xr_ps_of[s][:]),
-                    scalar=slope[:, t : t + 1],
-                    in1=diff_of[s][:, t, :].rearrange("p (c i) -> p c i", i=RUN),
-                    op0=ALU.mult,
-                    op1=ALU.add,
-                )
+                add_slope(s, t)
+
+        def square(s, t, half=None):
+            nc.scalar.activation(
+                out=squares_tile(s)[:, run_range(half), t, :],
+                in_=spread_x(s, half),
+                func=ACT.Square,
+                bias=neg_grid[:, t : t + 1],
+                scale=1.0,
+            )
 
         def scalar_squares(s):
-            sq = squares_tile(s)
             for t in scalar_planes(s):
-                nc.scalar.activation(
-                    out=sq[:, :, t, :],
-                    in_=runs(xr_ps_of[s][:]),
-                    func=ACT.Square,
-                    bias=neg_grid[:, t : t + 1],
-                    scale=1.0,
-                )
+                square(s, t)
 
-        def exponentials(s):
+        def exponentials(s, which=None):
             sq = sq_of[s]
-            basis = basis_pool.tile([P, PAIR, CHUNK, PACK], BF16, align_bytes=64)
-            for half, j0, n in pieces(s):
+            if s not in basis_of:
+                basis_of[s] = basis_pool.tile([P, PAIR, CHUNK, PACK], BF16, align_bytes=64, name="basis")
+            basis = basis_of[s]
+            for half, j0, n in pieces(s) if which is None else [pieces(s)[which]]:
                 first = (half * CHUNK + j0 * P) // RUN
                 nc.scalar.activation(
                     out=basis[:, half, j0 * P : (j0 + n) * P, :].rearrange("p (c i) t -> p c t i", i=RUN),
@@ -216,7 +235,6 @@ def tile_gaussiankernel_kernel(tc, x, grid, spline_weight_words, spline_weight_s
                     func=ACT.Exp,
                     scale=-INV_H2,
                 )
-            basis_of[s] = basis
 
         def quantise(s):
             basis = basis_of[s]
@@ -264,7 +282,33 @@ def tile_gaussiankernel_kernel(tc, x, grid, spline_weight_words, spline_weight_s
         def valid(s):
             return 0 <= s < STEPS
 
-        for k in range(-4, STEPS + 2):
+        last_plane = PACK - 1
+        for s in range(2):
+            transpose_features(s)
+            copy_transposed(s)
+            spread_features(s)
+        square(0, last_plane, 0)
+        square(0, last_plane - 1, 0)
+        square(0, last_plane, 1)
+        for t in range(last_plane - 1):
+            add_constant(nc.vector, 0, t, 0)
+        for t in range(last_plane - 1):
+            add_slope(0, t, 0)
+        scalar_squares(1)
+        add_constant(nc.gpsimd, 0, last_plane - 1, 1)
+        gpsimd_constants(1)
+        exponentials(0, 0)
+        transpose_features(2)
+        copy_transposed(2)
+        spread_features(2)
+        for t in range(last_plane - 1):
+            add_constant(nc.vector, 0, t, 1)
+        for t in range(last_plane):
+            add_slope(0, t, 1)
+        transpose_features(3)
+        copy_transposed(3)
+
+        for k in range(STEPS + 2):
             if valid(k + 3):
                 spread_features(k + 3)
             if valid(k + 4):
@@ -279,7 +323,7 @@ def tile_gaussiankernel_kernel(tc, x, grid, spline_weight_words, spline_weight_s
             if valid(k + 4):
                 copy_transposed(k + 4)
             if valid(k):
-                exponentials(k)
+                exponentials(k, 1 if k == 0 else None)
             if valid(k - 1):
                 quantise(k - 1)
             if valid(k - 2) and (k - 1) % STEPS_PER_CHUNK == 0:

@@ -20,13 +20,18 @@ PASSES = FEATURES * GRID // K_PASS
 INV_H2 = 49.0 / 16.0
 
 ROW_TILES = BATCH // P
-CHUNK_TILES = 4
+CHUNK_TILES = 2
 CHUNK = CHUNK_TILES * P
 PAIR = 2
-STEPS_PER_CHUNK = PASSES // PAIR
+BLOCKS = 2
+STEP_FEATURES = BLOCKS * P
+STEPS_PER_CHUNK = FEATURES // STEP_FEATURES
 CHUNKS = ROW_TILES // CHUNK_TILES
 STEPS = CHUNKS * STEPS_PER_CHUNK
-STEP_COLS = PAIR * CHUNK
+HALF_COLS = BLOCKS * CHUNK
+STEP_COLS = PAIR * HALF_COLS
+HALVED = 3
+FIRST_LOADS = 4
 RUN = 4
 
 FLOPS = 2 * BATCH * FEATURES * GRID * OUT
@@ -42,8 +47,11 @@ def vector_planes(s):
 
 def pieces(s):
     if s == STEPS - 1:
-        return [(0, 0, CHUNK_TILES)] + [(1, j, 1) for j in range(CHUNK_TILES)]
-    return [(half, 0, CHUNK_TILES) for half in range(PAIR)]
+        tail = STEP_COLS - CHUNK
+        return [(0, HALF_COLS), (HALF_COLS, HALF_COLS - CHUNK)] + [(tail + j * P, P) for j in range(CHUNK_TILES)]
+    if s == 0 or s >= STEPS - HALVED:
+        return [(half * HALF_COLS, HALF_COLS) for half in range(PAIR)]
+    return [(0, STEP_COLS)]
 
 
 def tile_gaussiankernel_kernel(tc, x, grid, spline_weight_words, spline_weight_scales, out):
@@ -69,7 +77,7 @@ def tile_gaussiankernel_kernel(tc, x, grid, spline_weight_words, spline_weight_s
         def load_x(s):
             chunk, part = divmod(s, STEPS_PER_CHUNK)
             rows = slice(chunk * CHUNK_TILES, (chunk + 1) * CHUNK_TILES)
-            cols = slice(part * P, (part + 1) * P)
+            cols = slice(part * STEP_FEATURES, (part + 1) * STEP_FEATURES)
             nc.sync.dma_start(out=x_sb[:, rows, cols], in_=x_rows[:, rows, cols])
 
         load_x(0)
@@ -85,7 +93,7 @@ def tile_gaussiankernel_kernel(tc, x, grid, spline_weight_words, spline_weight_s
         with nc.allow_non_contiguous_dma(reason="eight bytes of the grid to each partition"):
             nc.sync.dma_start(out=grid_bf[0:P:2, :], in_=grid[0:PACK].partition_broadcast(P // 2))
             nc.sync.dma_start(out=grid_bf[1:P:2, :], in_=grid[PACK:GRID].partition_broadcast(P // 2))
-        for s in range(1, STEPS_PER_CHUNK):
+        for s in range(1, FIRST_LOADS):
             load_x(s)
 
         for quad in range(4):
@@ -103,7 +111,7 @@ def tile_gaussiankernel_kernel(tc, x, grid, spline_weight_words, spline_weight_s
 
         for g in range(PASSES):
             load_weight(g)
-        for s in range(STEPS_PER_CHUNK, STEPS):
+        for s in range(FIRST_LOADS, STEPS):
             load_x(s)
 
         ident = keep.tile([P, P], BF16)
@@ -133,25 +141,27 @@ def tile_gaussiankernel_kernel(tc, x, grid, spline_weight_words, spline_weight_s
 
         def transpose_features(s):
             chunk, part = divmod(s, STEPS_PER_CHUNK)
-            xt_ps = xt_psum.tile([P, CHUNK], BF16)
-            for j in range(CHUNK_TILES):
-                nc.tensor.transpose(
-                    xt_ps[:, j * P : (j + 1) * P],
-                    x_sb[:, chunk * CHUNK_TILES + j, part * P : (part + 1) * P],
-                    ident[:],
-                )
+            xt_ps = xt_psum.tile([P, BLOCKS, CHUNK], BF16)
+            for block in range(BLOCKS):
+                feature = part * STEP_FEATURES + block * P
+                for j in range(CHUNK_TILES):
+                    nc.tensor.transpose(
+                        xt_ps[:, block, j * P : (j + 1) * P],
+                        x_sb[:, chunk * CHUNK_TILES + j, feature : feature + P],
+                        ident[:],
+                    )
             xt_ps_of[s] = xt_ps
 
         def copy_transposed(s):
-            xt = xt_pool.tile([P, CHUNK], BF16)
-            nc.vector.tensor_copy(out=xt[:], in_=xt_ps_of[s][:])
+            xt = xt_pool.tile([P, HALF_COLS], BF16)
+            nc.vector.tensor_copy(out=xt[:], in_=xt_ps_of[s][:].rearrange("p k b -> p (k b)"))
             xt_of[s] = xt
 
         def spread_features(s):
-            xr_ps = xr_psum.tile([P, PAIR, CHUNK], BF16)
+            xr_ps = xr_psum.tile([P, PAIR, HALF_COLS], BF16)
             halves = [xr_ps[:, half, :] for half in range(PAIR)]
             if s == 0:
-                second = acc_psum.tile([P, CHUNK], BF16, name="first_x", tag="acc_%d" % (CHUNK_TILES - 1))
+                second = acc_psum.tile([P, HALF_COLS], BF16, name="first_x", tag="acc_%d" % (2 * CHUNK_TILES - 1))
                 halves[1] = second[:]
             xt = xt_of[s]
             for half in range(PAIR):
@@ -171,7 +181,7 @@ def tile_gaussiankernel_kernel(tc, x, grid, spline_weight_words, spline_weight_s
             return halves_of[s][half].rearrange("p (c i) -> p c i", i=RUN)
 
         def run_range(half):
-            per_half = CHUNK // RUN
+            per_half = HALF_COLS // RUN
             return slice(0, PAIR * per_half) if half is None else slice(half * per_half, (half + 1) * per_half)
 
         def squares_tile(s):
@@ -225,59 +235,62 @@ def tile_gaussiankernel_kernel(tc, x, grid, spline_weight_words, spline_weight_s
         def exponentials(s, which=None):
             sq = sq_of[s]
             if s not in basis_of:
-                basis_of[s] = basis_pool.tile([P, PAIR, CHUNK, PACK], BF16, align_bytes=64, name="basis")
+                basis_of[s] = basis_pool.tile([P, STEP_COLS, PACK], BF16, align_bytes=64, name="basis")
             basis = basis_of[s]
-            for half, j0, n in pieces(s) if which is None else [pieces(s)[which]]:
-                first = (half * CHUNK + j0 * P) // RUN
+            for first, n in pieces(s) if which is None else [pieces(s)[which]]:
                 nc.scalar.activation(
-                    out=basis[:, half, j0 * P : (j0 + n) * P, :].rearrange("p (c i) t -> p c t i", i=RUN),
-                    in_=sq[:, first : first + n * P // RUN, :, :],
+                    out=basis[:, first : first + n, :].rearrange("p (c i) t -> p c t i", i=RUN),
+                    in_=sq[:, first // RUN : (first + n) // RUN, :, :],
                     func=ACT.Exp,
                     scale=-INV_H2,
                 )
 
         def quantise(s):
             basis = basis_of[s]
-            codes = mx_pool.tile([P, PAIR, CHUNK], U32, align_bytes=64)
-            scales = mx_pool.tile([P, PAIR, CHUNK], U8, align_bytes=64)
-            for half, j0, n in pieces(s):
-                cols = slice(j0 * P, (j0 + n) * P)
+            codes = mx_pool.tile([P, STEP_COLS], U32, align_bytes=64)
+            scales = mx_pool.tile([P, STEP_COLS], U8, align_bytes=64)
+            for first, n in pieces(s):
+                cols = slice(first, first + n)
                 nc.vector.quantize_mx(
-                    out=codes[:, half, cols].bitcast(FP8X4),
-                    scales=scales[:, half, cols],
-                    in_=basis[:, half, cols, :].rearrange("p b t -> p (b t)"),
+                    out=codes[:, cols].bitcast(FP8X4),
+                    scales=scales[:, cols],
+                    in_=basis[:, cols, :].rearrange("p b t -> p (b t)"),
                 )
             codes_of[s] = codes
             scales_of[s] = scales
 
         def multiply(s):
-            part = s % STEPS_PER_CHUNK
+            chunk, part = divmod(s, STEPS_PER_CHUNK)
             codes = codes_of[s]
             scales = scales_of[s]
-            for half in range(PAIR):
-                g = part * PAIR + half
+            order = [(half, block) for half in range(PAIR) for block in range(BLOCKS)]
+            for half, block in order:
+                g = (part * BLOCKS + block) * PAIR + half
+                first = part == 0 and (half, block) == order[0]
+                last = part == STEPS_PER_CHUNK - 1 and (half, block) == order[-1]
                 for j in range(CHUNK_TILES):
-                    if g == 0:
-                        acc_of[j] = acc_psum.tile([P, OUT], F32, name="acc_%d" % j, tag="acc_%d" % j)
-                    cols = slice(j * P, (j + 1) * P)
+                    if first:
+                        name = "acc_%d" % (chunk % 2 * CHUNK_TILES + j)
+                        acc_of[chunk, j] = acc_psum.tile([P, OUT], F32, name=name, tag=name)
+                    col = half * HALF_COLS + block * CHUNK + j * P
+                    cols = slice(col, col + P)
                     nc.tensor.matmul_mx(
-                        out=acc_of[j][:],
-                        lhsT=codes[:, half, cols].bitcast(FP8X4),
-                        lhsT_scale=scales[:, half, cols],
+                        out=acc_of[chunk, j][:],
+                        lhsT=codes[:, cols].bitcast(FP8X4),
+                        lhsT_scale=scales[:, cols],
                         rhs=w_words[:, g, :].bitcast(FP8X4),
                         rhs_scale=w_scales[:, g, :],
-                        start=(g == 0),
-                        stop=(g == PASSES - 1),
+                        start=first,
+                        stop=last,
                     )
 
-        def store_chunk(chunk):
-            for j in range(CHUNK_TILES):
-                res = res_pool.tile([P, OUT], F32)
-                if chunk == CHUNKS - 1 and j % 2 == 1:
-                    nc.scalar.copy(out=res[:], in_=acc_of[j][:])
-                else:
-                    nc.vector.tensor_copy(out=res[:], in_=acc_of[j][:])
-                nc.sync.dma_start(out=out_rows[:, chunk * CHUNK_TILES + j, :], in_=res[:])
+        def store_tile(chunk, j):
+            res = res_pool.tile([P, OUT], F32)
+            if chunk == CHUNKS - 1 and j == CHUNK_TILES - 1:
+                nc.scalar.copy(out=res[:], in_=acc_of[chunk, j][:])
+            else:
+                nc.vector.tensor_copy(out=res[:], in_=acc_of[chunk, j][:])
+            nc.sync.dma_start(out=out_rows[:, chunk * CHUNK_TILES + j, :], in_=res[:])
 
         def valid(s):
             return 0 <= s < STEPS
@@ -308,7 +321,7 @@ def tile_gaussiankernel_kernel(tc, x, grid, spline_weight_words, spline_weight_s
         transpose_features(3)
         copy_transposed(3)
 
-        for k in range(STEPS + 2):
+        for k in range(STEPS + 3):
             if valid(k + 3):
                 spread_features(k + 3)
             if valid(k + 4):
@@ -326,5 +339,7 @@ def tile_gaussiankernel_kernel(tc, x, grid, spline_weight_words, spline_weight_s
                 exponentials(k, 1 if k == 0 else None)
             if valid(k - 1):
                 quantise(k - 1)
-            if valid(k - 2) and (k - 1) % STEPS_PER_CHUNK == 0:
-                store_chunk((k - 1) // STEPS_PER_CHUNK - 1)
+            for j in range(CHUNK_TILES):
+                s = k - 2 - j
+                if valid(s) and s % STEPS_PER_CHUNK == STEPS_PER_CHUNK - 1:
+                    store_tile(s // STEPS_PER_CHUNK, j)

@@ -31,6 +31,7 @@ STEPS = CHUNKS * STEPS_PER_CHUNK
 HALF_COLS = BLOCKS * CHUNK
 STEP_COLS = PAIR * HALF_COLS
 HALVED = 3
+TWICE = 2
 FIRST_LOADS = 4
 RUN = 4
 
@@ -122,6 +123,21 @@ def tile_gaussiankernel_kernel(tc, x, grid, spline_weight_words, spline_weight_s
                 out=spread[:, half, :, :],
                 in_=ident[:, 64 * half : 64 * half + 64].unsqueeze(2).to_broadcast([P, P // 2, 2]),
             )
+        twice = keep.tile([P, TWICE, PAIR, CHUNK_TILES, BLOCKS, P // 2, 2], BF16)
+
+        def x_of_half(s, half, j):
+            part = x_sb[:, j, s * STEP_FEATURES : (s + 1) * STEP_FEATURES]
+            part = part.rearrange("p (k h i) -> p k h i", k=BLOCKS, h=PAIR)[:, :, half, :]
+            return part.unsqueeze(3).to_broadcast([P, BLOCKS, P // 2, 2])
+
+        def lay_twice(s):
+            for j in range(CHUNK_TILES):
+                nc.vector.tensor_copy(out=twice[:, s, 0, j, :, :, :], in_=x_of_half(s, 0, j))
+                nc.gpsimd.tensor_scalar(
+                    out=twice[:, s, 1, j, :, :, :], in0=x_of_half(s, 1, j), scalar1=1.0, scalar2=0.0, op0=ALU.mult, op1=ALU.add
+                )
+
+        lay_twice(0)
         neg_grid = keep.tile([P, PACK], F32)
         nc.vector.tensor_scalar_mul(out=neg_grid[:], in0=grid_bf[:], scalar1=-1.0)
         last = neg_grid[:, PACK - 1 : PACK]
@@ -157,23 +173,35 @@ def tile_gaussiankernel_kernel(tc, x, grid, spline_weight_words, spline_weight_s
             nc.vector.tensor_copy(out=xt[:], in_=xt_ps_of[s][:].rearrange("p k b -> p (k b)"))
             xt_of[s] = xt
 
-        def spread_features(s):
+        def transpose_twice(s):
             xr_ps = xr_psum.tile([P, PAIR, HALF_COLS], BF16)
-            halves = [xr_ps[:, half, :] for half in range(PAIR)]
+            xr_ps_of[s] = xr_ps
+            halves_of[s] = [xr_ps[:, half, :] for half in range(PAIR)]
             if s == 0:
                 second = acc_psum.tile([P, HALF_COLS], BF16, name="first_x", tag="acc_%d" % (2 * CHUNK_TILES - 1))
-                halves[1] = second[:]
+                halves_of[s][1] = second[:]
+            for half in range(PAIR):
+                for j in range(CHUNK_TILES):
+                    for block in range(BLOCKS):
+                        col = block * CHUNK + j * P
+                        nc.tensor.transpose(
+                            halves_of[s][half][:, col : col + P],
+                            twice[:, s, half, j, block, :, :].rearrange("p i c -> p (i c)"),
+                            ident[:],
+                        )
+
+        def spread_features(s):
+            xr_ps = xr_psum.tile([P, PAIR, HALF_COLS], BF16)
             xt = xt_of[s]
             for half in range(PAIR):
                 nc.tensor.matmul(
-                    out=halves[half],
+                    out=xr_ps[:, half, :],
                     lhsT=spread[:, half, :, :].rearrange("p i c -> p (i c)"),
                     rhs=xt[:],
                     start=True,
                     stop=True,
                 )
             xr_ps_of[s] = xr_ps
-            halves_of[s] = halves
 
         def spread_x(s, half):
             if half is None:
@@ -296,10 +324,9 @@ def tile_gaussiankernel_kernel(tc, x, grid, spline_weight_words, spline_weight_s
             return 0 <= s < STEPS
 
         last_plane = PACK - 1
-        for s in range(2):
-            transpose_features(s)
-            copy_transposed(s)
-            spread_features(s)
+        transpose_twice(0)
+        lay_twice(1)
+        transpose_twice(1)
         square(0, last_plane, 0)
         square(0, last_plane - 1, 0)
         square(0, last_plane, 1)

@@ -21,14 +21,14 @@ INV_H2 = 49.0 / 16.0
 
 ROW_TILES = BATCH // P
 CHUNK_TILES = 2
-CHUNK = CHUNK_TILES * P
 PAIR = 2
 BLOCKS = 2
 STEP_FEATURES = BLOCKS * P
 STEPS_PER_CHUNK = FEATURES // STEP_FEATURES
 CHUNKS = ROW_TILES // CHUNK_TILES
 STEPS = CHUNKS * STEPS_PER_CHUNK
-HALF_COLS = BLOCKS * CHUNK
+TILE_COLS = BLOCKS * P
+HALF_COLS = CHUNK_TILES * TILE_COLS
 STEP_COLS = PAIR * HALF_COLS
 HALVED = 3
 TWICE = 2
@@ -48,8 +48,8 @@ def vector_planes(s):
 
 def pieces(s):
     if s == STEPS - 1:
-        tail = STEP_COLS - CHUNK
-        return [(0, HALF_COLS), (HALF_COLS, HALF_COLS - CHUNK)] + [(tail + j * P, P) for j in range(CHUNK_TILES)]
+        tail = STEP_COLS - TILE_COLS
+        return [(0, HALF_COLS), (HALF_COLS, HALF_COLS - TILE_COLS)] + [(tail + k * P, P) for k in range(BLOCKS)]
     if s == 0 or s >= STEPS - HALVED:
         return [(half * HALF_COLS, HALF_COLS) for half in range(PAIR)]
     return [(0, STEP_COLS)]
@@ -157,12 +157,12 @@ def tile_gaussiankernel_kernel(tc, x, grid, spline_weight_words, spline_weight_s
 
         def transpose_features(s):
             chunk, part = divmod(s, STEPS_PER_CHUNK)
-            xt_ps = xt_psum.tile([P, BLOCKS, CHUNK], BF16)
-            for block in range(BLOCKS):
-                feature = part * STEP_FEATURES + block * P
-                for j in range(CHUNK_TILES):
+            xt_ps = xt_psum.tile([P, CHUNK_TILES, BLOCKS, P], BF16)
+            for j in range(CHUNK_TILES):
+                for block in range(BLOCKS):
+                    feature = part * STEP_FEATURES + block * P
                     nc.tensor.transpose(
-                        xt_ps[:, block, j * P : (j + 1) * P],
+                        xt_ps[:, j, block, :],
                         x_sb[:, chunk * CHUNK_TILES + j, feature : feature + P],
                         ident[:],
                     )
@@ -170,7 +170,7 @@ def tile_gaussiankernel_kernel(tc, x, grid, spline_weight_words, spline_weight_s
 
         def copy_transposed(s):
             xt = xt_pool.tile([P, HALF_COLS], BF16)
-            nc.vector.tensor_copy(out=xt[:], in_=xt_ps_of[s][:].rearrange("p k b -> p (k b)"))
+            nc.vector.tensor_copy(out=xt[:], in_=xt_ps_of[s][:].rearrange("p j k b -> p (j k b)"))
             xt_of[s] = xt
 
         def transpose_twice(s):
@@ -183,7 +183,7 @@ def tile_gaussiankernel_kernel(tc, x, grid, spline_weight_words, spline_weight_s
             for half in range(PAIR):
                 for j in range(CHUNK_TILES):
                     for block in range(BLOCKS):
-                        col = block * CHUNK + j * P
+                        col = j * TILE_COLS + block * P
                         nc.tensor.transpose(
                             halves_of[s][half][:, col : col + P],
                             twice[:, s, half, j, block, :, :].rearrange("p i c -> p (i c)"),
@@ -291,30 +291,35 @@ def tile_gaussiankernel_kernel(tc, x, grid, spline_weight_words, spline_weight_s
             chunk, part = divmod(s, STEPS_PER_CHUNK)
             codes = codes_of[s]
             scales = scales_of[s]
-            order = [(half, block) for half in range(PAIR) for block in range(BLOCKS)]
-            for half, block in order:
-                g = (part * BLOCKS + block) * PAIR + half
-                first = part == 0 and (half, block) == order[0]
-                last = part == STEPS_PER_CHUNK - 1 and (half, block) == order[-1]
+            for half in range(PAIR):
                 for j in range(CHUNK_TILES):
-                    if first:
-                        name = "acc_%d" % (chunk % 2 * CHUNK_TILES + j)
-                        acc_of[chunk, j] = acc_psum.tile([P, OUT], F32, name=name, tag=name)
-                    col = half * HALF_COLS + block * CHUNK + j * P
-                    cols = slice(col, col + P)
-                    nc.tensor.matmul_mx(
-                        out=acc_of[chunk, j][:],
-                        lhsT=codes[:, cols].bitcast(FP8X4),
-                        lhsT_scale=scales[:, cols],
-                        rhs=w_words[:, g, :].bitcast(FP8X4),
-                        rhs_scale=w_scales[:, g, :],
-                        start=first,
-                        stop=last,
-                    )
+                    for block in range(BLOCKS):
+                        g = (part * BLOCKS + block) * PAIR + half
+                        first = part == 0 and half == 0 and block == 0
+                        last = part == STEPS_PER_CHUNK - 1 and half == PAIR - 1 and block == BLOCKS - 1
+                        if first:
+                            name = "acc_%d" % (chunk % 2 * CHUNK_TILES + j)
+                            acc_of[chunk, j] = acc_psum.tile([P, OUT], F32, name=name, tag=name)
+                        col = half * HALF_COLS + j * TILE_COLS + block * P
+                        cols = slice(col, col + P)
+                        nc.tensor.matmul_mx(
+                            out=acc_of[chunk, j][:],
+                            lhsT=codes[:, cols].bitcast(FP8X4),
+                            lhsT_scale=scales[:, cols],
+                            rhs=w_words[:, g, :].bitcast(FP8X4),
+                            rhs_scale=w_scales[:, g, :],
+                            start=first,
+                            stop=last,
+                        )
 
         def store_tile(chunk, j):
             res = res_pool.tile([P, OUT], F32)
             if chunk == CHUNKS - 1 and j == CHUNK_TILES - 1:
+                for cols in (slice(0, OUT // 2), slice(OUT // 2, OUT)):
+                    nc.scalar.copy(out=res[:, cols], in_=acc_of[chunk, j][:, cols])
+                    nc.sync.dma_start(out=out_rows[:, chunk * CHUNK_TILES + j, cols], in_=res[:, cols])
+                return
+            if chunk == CHUNKS - 2 and j == CHUNK_TILES - 1:
                 nc.scalar.copy(out=res[:], in_=acc_of[chunk, j][:])
             else:
                 nc.vector.tensor_copy(out=res[:], in_=acc_of[chunk, j][:])
@@ -367,6 +372,8 @@ def tile_gaussiankernel_kernel(tc, x, grid, spline_weight_words, spline_weight_s
             if valid(k - 1):
                 quantise(k - 1)
             for j in range(CHUNK_TILES):
-                s = k - 2 - j
-                if valid(s) and s % STEPS_PER_CHUNK == STEPS_PER_CHUNK - 1:
-                    store_tile(s // STEPS_PER_CHUNK, j)
+                for chunk in range(CHUNKS):
+                    last_step = (chunk + 1) * STEPS_PER_CHUNK - 1
+                    delay = 1 if (chunk, j) == (CHUNKS - 3, 0) else j
+                    if k == last_step + 2 + delay:
+                        store_tile(chunk, j)

@@ -365,12 +365,12 @@ def tile_gaussiankernel_kernel(tc, x, grid, spline_weight_words, spline_weight_s
                 gpsimd_constants(k + 2)
             if valid(k + 1):
                 vector_squares(k + 1)
-            if valid(k + 4):
-                copy_transposed(k + 4)
             if valid(k):
                 exponentials(k, 1 if k == 0 else None)
             if valid(k - 1):
                 quantise(k - 1)
+            if valid(k + 4):
+                copy_transposed(k + 4)
             for j in range(CHUNK_TILES):
                 for chunk in range(CHUNKS):
                     last_step = (chunk + 1) * STEPS_PER_CHUNK - 1

from contextlib import ExitStack

import concourse.mybir as mybir
from concourse.masks import make_identity

F32 = mybir.dt.float32
BF16 = mybir.dt.bfloat16
I32 = mybir.dt.int32
U32 = mybir.dt.uint32
U8 = mybir.dt.uint8
FP8X4 = mybir.dt.float8_e4m3fn_x4
ACT = mybir.ActivationFunctionType
ALU = mybir.AluOpType

P = 128
PACK = 4
BATCH, FEATURES, GRID, OUT = 2048, 512, 8, 512
K_PASS = P * PACK
PASSES = FEATURES * GRID // K_PASS
INV_H2 = 49.0 / 16.0

ROW_TILES = BATCH // P
CHUNK_TILES = 2
PAIR = 2
BLOCKS = 2
STEP_FEATURES = BLOCKS * P
STEPS_PER_CHUNK = FEATURES // STEP_FEATURES
CHUNKS = ROW_TILES // CHUNK_TILES
STEPS = CHUNKS * STEPS_PER_CHUNK
TILE_COLS = BLOCKS * P
HALF_COLS = CHUNK_TILES * TILE_COLS
STEP_COLS = PAIR * HALF_COLS
HALVED = 3
TWICE = 2
FIRST_LOADS = 4
RUN = 4

FLOPS = 2 * BATCH * FEATURES * GRID * OUT


def scalar_planes(s):
    return (PACK - 1,)


def vector_planes(s):
    return tuple([t for t in range(PACK) if t not in scalar_planes(s)])


def pieces(s):
    if s == STEPS - 1:
        tail = STEP_COLS - TILE_COLS
        return [(0, HALF_COLS), (HALF_COLS, HALF_COLS - TILE_COLS)] + [(tail + k * P, P) for k in range(BLOCKS)]
    if s == 0 or s >= STEPS - HALVED:
        return [(half * HALF_COLS, HALF_COLS) for half in range(PAIR)]
    return [(0, STEP_COLS)]


def tile_gaussiankernel_kernel(tc, x, grid, spline_weight_words, spline_weight_scales, out):
    nc = tc.nc
    x_rows = x.rearrange("(p r) i -> p r i", r=ROW_TILES)
    out_rows = out.rearrange("(p r) n -> p r n", r=ROW_TILES)

    with ExitStack() as ctx:
        keep = ctx.enter_context(tc.tile_pool(name="keep", bufs=1))
        xt_pool = ctx.enter_context(tc.tile_pool(name="xt", bufs=2))
        diff_pool = ctx.enter_context(tc.tile_pool(name="diff", bufs=3))
        sq_pool = ctx.enter_context(tc.tile_pool(name="sq", bufs=4))
        basis_pool = ctx.enter_context(tc.tile_pool(name="basis", bufs=3))
        mx_pool = ctx.enter_context(tc.tile_pool(name="mx", bufs=3))
        res_pool = ctx.enter_context(tc.tile_pool(name="res", bufs=4))
        xt_psum = ctx.enter_context(tc.psum_pool(name="xt_psum", bufs=1))
        xr_psum = ctx.enter_context(tc.psum_pool(name="xr_psum", bufs=3))
        acc_psum = ctx.enter_context(tc.psum_pool(name="acc_psum", bufs=1))
        ctx.enter_context(tc.manual_schedule())

        x_sb = keep.tile([P, ROW_TILES, FEATURES], BF16)

        def load_x(s):
            chunk, part = divmod(s, STEPS_PER_CHUNK)
            rows = slice(chunk * CHUNK_TILES, (chunk + 1) * CHUNK_TILES)
            cols = slice(part * STEP_FEATURES, (part + 1) * STEP_FEATURES)
            nc.sync.dma_start(out=x_sb[:, rows, cols], in_=x_rows[:, rows, cols])

        load_x(0)

        warm = keep.tile([P, 2], F32)
        nc.vector.memset(warm[:], 0.0)
        nc.scalar.activation(out=warm[:, 1:2], in_=warm[:, 0:1], func=ACT.Exp)

        w_scales = keep.tile([P, PASSES, OUT], U8, align_bytes=64)
        nc.vector.memset(w_scales[:].rearrange("p g n -> p (g n)").bitcast(I32), 0)

        grid_bf = keep.tile([P, PACK], BF16)
        with nc.allow_non_contiguous_dma(reason="eight bytes of the grid to each partition"):
            nc.sync.dma_start(out=grid_bf[0:P:2, :], in_=grid[0:PACK].partition_broadcast(P // 2))
            nc.sync.dma_start(out=grid_bf[1:P:2, :], in_=grid[PACK:GRID].partition_broadcast(P // 2))
        for s in range(1, FIRST_LOADS):
            load_x(s)

        for quad in range(4):
            nc.sync.dma_start(
                out=w_scales[32 * quad : 32 * quad + 4, :, :].bitcast(I32),
                in_=spline_weight_scales[:, 4 * quad : 4 * quad + 4, :].rearrange("g r n -> r g n").bitcast(I32),
            )
        w_words = keep.tile([P, PASSES, OUT], U32, align_bytes=64)

        def load_weight(g):
            nc.sync.dma_start(
                out=w_words[:, g, :].bitcast(I32),
                in_=spline_weight_words[g].rearrange("p n t -> p (n t)").bitcast(I32),
            )

        for g in range(PASSES):
            load_weight(g)
        for s in range(FIRST_LOADS, STEPS):
            load_x(s)

        ident = keep.tile([P, P], BF16)
        make_identity(nc, ident[:])
        spread = keep.tile([P, PAIR, P // 2, 2], BF16)
        for half in range(PAIR):
            nc.vector.tensor_copy(
                out=spread[:, half, :, :],
                in_=ident[:, 64 * half : 64 * half + 64].unsqueeze(2).to_broadcast([P, P // 2, 2]),
            )
        twice = keep.tile([P, TWICE, PAIR, CHUNK_TILES, BLOCKS, P // 2, 2], BF16)

        def x_of_half(s, half, j):
            part = x_sb[:, j, s * STEP_FEATURES : (s + 1) * STEP_FEATURES]
            part = part.rearrange("p (k h i) -> p k h i", k=BLOCKS, h=PAIR)[:, :, half, :]
            return part.unsqueeze(3).to_broadcast([P, BLOCKS, P // 2, 2])

        def lay_twice(s):
            for j in range(CHUNK_TILES):
                nc.vector.tensor_copy(out=twice[:, s, 0, j, :, :, :], in_=x_of_half(s, 0, j))
                nc.gpsimd.tensor_scalar(
                    out=twice[:, s, 1, j, :, :, :], in0=x_of_half(s, 1, j), scalar1=1.0, scalar2=0.0, op0=ALU.mult, op1=ALU.add
                )

        lay_twice(0)
        neg_grid = keep.tile([P, PACK], F32)
        nc.vector.tensor_scalar_mul(out=neg_grid[:], in0=grid_bf[:], scalar1=-1.0)
        last = neg_grid[:, PACK - 1 : PACK]
        step_to_last = keep.tile([P, PACK - 1], F32)
        slope = keep.tile([P, PACK - 1], F32)
        constant = keep.tile([P, PACK - 1], F32)
        nc.vector.tensor_scalar(
            out=step_to_last[:], in0=neg_grid[:, 0 : PACK - 1], scalar1=last, scalar2=1.0, op0=ALU.subtract, op1=ALU.mult
        )
        nc.vector.tensor_scalar_mul(out=slope[:], in0=step_to_last[:], scalar1=2.0)
        nc.vector.scalar_tensor_tensor(
            out=constant[:], in0=neg_grid[:, 0 : PACK - 1], scalar=last, in1=step_to_last[:], op0=ALU.add, op1=ALU.mult
        )

        xt_ps_of, xt_of, xr_ps_of, halves_of, diff_of, sq_of, basis_of = {}, {}, {}, {}, {}, {}, {}
        codes_of, scales_of, acc_of = {}, {}, {}

        def transpose_features(s):
            chunk, part = divmod(s, STEPS_PER_CHUNK)
            xt_ps = xt_psum.tile([P, CHUNK_TILES, BLOCKS, P], BF16)
            for j in range(CHUNK_TILES):
                for block in range(BLOCKS):
                    feature = part * STEP_FEATURES + block * P
                    nc.tensor.transpose(
                        xt_ps[:, j, block, :],
                        x_sb[:, chunk * CHUNK_TILES + j, feature : feature + P],
                        ident[:],
                    )
            xt_ps_of[s] = xt_ps

        def copy_transposed(s):
            xt = xt_pool.tile([P, HALF_COLS], BF16)
            nc.vector.tensor_copy(out=xt[:], in_=xt_ps_of[s][:].rearrange("p j k b -> p (j k b)"))
            xt_of[s] = xt

        def transpose_twice(s):
            xr_ps = xr_psum.tile([P, PAIR, HALF_COLS], BF16)
            xr_ps_of[s] = xr_ps
            halves_of[s] = [xr_ps[:, half, :] for half in range(PAIR)]
            if s == 0:
                second = acc_psum.tile([P, HALF_COLS], BF16, name="first_x", tag="acc_%d" % (2 * CHUNK_TILES - 1))
                halves_of[s][1] = second[:]
            for half in range(PAIR):
                for j in range(CHUNK_TILES):
                    for block in range(BLOCKS):
                        col = j * TILE_COLS + block * P
                        nc.tensor.transpose(
                            halves_of[s][half][:, col : col + P],
                            twice[:, s, half, j, block, :, :].rearrange("p i c -> p (i c)"),
                            ident[:],
                        )

        def spread_features(s):
            xr_ps = xr_psum.tile([P, PAIR, HALF_COLS], BF16)
            xt = xt_of[s]
            for half in range(PAIR):
                nc.tensor.matmul(
                    out=xr_ps[:, half, :],
                    lhsT=spread[:, half, :, :].rearrange("p i c -> p (i c)"),
                    rhs=xt[:],
                    start=True,
                    stop=True,
                )
            xr_ps_of[s] = xr_ps

        def spread_x(s, half):
            if half is None:
                return xr_ps_of[s][:].rearrange("p h b -> p (h b)").rearrange("p (c i) -> p c i", i=RUN)
            return halves_of[s][half].rearrange("p (c i) -> p c i", i=RUN)

        def run_range(half):
            per_half = HALF_COLS // RUN
            return slice(0, PAIR * per_half) if half is None else slice(half * per_half, (half + 1) * per_half)

        def squares_tile(s):
            if s not in sq_of:
                sq_of[s] = sq_pool.tile([P, STEP_COLS // RUN, PACK, RUN], F32, name="sq")
            return sq_of[s]

        def add_constant(engine, s, t, half=None):
            if (s, t) not in diff_of:
                diff_of[s, t] = diff_pool.tile([P, STEP_COLS // RUN, RUN], F32, name="diff_%d" % t, tag="diff_%d" % t)
            engine.tensor_scalar(
                out=diff_of[s, t][:, run_range(half), :],
                in0=sq_of[s][:, run_range(half), PACK - 1, :],
                scalar1=1.0,
                scalar2=constant[:, t : t + 1],
                op0=ALU.mult,
                op1=ALU.add,
            )

        def gpsimd_constants(s):
            for t in vector_planes(s):
                add_constant(nc.gpsimd, s, t)

        def add_slope(s, t, half=None):
            nc.vector.scalar_tensor_tensor(
                out=squares_tile(s)[:, run_range(half), t, :],
                in0=spread_x(s, half),
                scalar=slope[:, t : t + 1],
                in1=diff_of[s, t][:, run_range(half), :],
                op0=ALU.mult,
                op1=ALU.add,
            )

        def vector_squares(s):
            for t in vector_planes(s):
                add_slope(s, t)

        def square(s, t, half=None):
            nc.scalar.activation(
                out=squares_tile(s)[:, run_range(half), t, :],
                in_=spread_x(s, half),
                func=ACT.Square,
                bias=neg_grid[:, t : t + 1],
                scale=1.0,
            )

        def scalar_squares(s):
            for t in scalar_planes(s):
                square(s, t)

        def exponentials(s, which=None):
            sq = sq_of[s]
            if s not in basis_of:
                basis_of[s] = basis_pool.tile([P, STEP_COLS, PACK], BF16, align_bytes=64, name="basis")
            basis = basis_of[s]
            for first, n in pieces(s) if which is None else [pieces(s)[which]]:
                nc.scalar.activation(
                    out=basis[:, first : first + n, :].rearrange("p (c i) t -> p c t i", i=RUN),
                    in_=sq[:, first // RUN : (first + n) // RUN, :, :],
                    func=ACT.Exp,
                    scale=-INV_H2,
                )

        def quantise(s):
            basis = basis_of[s]
            codes = mx_pool.tile([P, STEP_COLS], U32, align_bytes=64)
            scales = mx_pool.tile([P, STEP_COLS], U8, align_bytes=64)
            for first, n in pieces(s):
                cols = slice(first, first + n)
                nc.vector.quantize_mx(
                    out=codes[:, cols].bitcast(FP8X4),
                    scales=scales[:, cols],
                    in_=basis[:, cols, :].rearrange("p b t -> p (b t)"),
                )
            codes_of[s] = codes
            scales_of[s] = scales

        def multiply(s):
            chunk, part = divmod(s, STEPS_PER_CHUNK)
            codes = codes_of[s]
            scales = scales_of[s]
            for half in range(PAIR):
                for j in range(CHUNK_TILES):
                    for block in range(BLOCKS):
                        g = (part * BLOCKS + block) * PAIR + half
                        first = part == 0 and half == 0 and block == 0
                        last = part == STEPS_PER_CHUNK - 1 and half == PAIR - 1 and block == BLOCKS - 1
                        if first:
                            name = "acc_%d" % (chunk % 2 * CHUNK_TILES + j)
                            acc_of[chunk, j] = acc_psum.tile([P, OUT], F32, name=name, tag=name)
                        col = half * HALF_COLS + j * TILE_COLS + block * P
                        cols = slice(col, col + P)
                        nc.tensor.matmul_mx(
                            out=acc_of[chunk, j][:],
                            lhsT=codes[:, cols].bitcast(FP8X4),
                            lhsT_scale=scales[:, cols],
                            rhs=w_words[:, g, :].bitcast(FP8X4),
                            rhs_scale=w_scales[:, g, :],
                            start=first,
                            stop=last,
                        )

        def store_tile(chunk, j):
            res = res_pool.tile([P, OUT], F32)
            if chunk == CHUNKS - 1 and j == CHUNK_TILES - 1:
                for cols in (slice(0, OUT // 2), slice(OUT // 2, OUT)):
                    nc.scalar.copy(out=res[:, cols], in_=acc_of[chunk, j][:, cols])
                    nc.sync.dma_start(out=out_rows[:, chunk * CHUNK_TILES + j, cols], in_=res[:, cols])
                return
            if chunk == CHUNKS - 2 and j == CHUNK_TILES - 1:
                nc.scalar.copy(out=res[:], in_=acc_of[chunk, j][:])
            else:
                nc.vector.tensor_copy(out=res[:], in_=acc_of[chunk, j][:])
            nc.sync.dma_start(out=out_rows[:, chunk * CHUNK_TILES + j, :], in_=res[:])

        def valid(s):
            return 0 <= s < STEPS

        last_plane = PACK - 1
        transpose_twice(0)
        lay_twice(1)
        transpose_twice(1)
        square(0, last_plane, 0)
        square(0, last_plane - 1, 0)
        square(0, last_plane, 1)
        for t in range(last_plane - 1):
            add_constant(nc.vector, 0, t, 0)
        for t in range(last_plane - 1):
            add_slope(0, t, 0)
        scalar_squares(1)
        add_constant(nc.gpsimd, 0, last_plane - 1, 1)
        gpsimd_constants(1)
        exponentials(0, 0)
        transpose_features(2)
        copy_transposed(2)
        spread_features(2)
        for t in range(last_plane - 1):
            add_constant(nc.vector, 0, t, 1)
        for t in range(last_plane):
            add_slope(0, t, 1)
        transpose_features(3)
        copy_transposed(3)

        for k in range(STEPS + 3):
            if valid(k + 3):
                spread_features(k + 3)
            if valid(k + 4):
                transpose_features(k + 4)
            if valid(k - 2):
                multiply(k - 2)
            if valid(k + 2):
                scalar_squares(k + 2)
                gpsimd_constants(k + 2)
            if valid(k + 1):
                vector_squares(k + 1)
            if valid(k):
                exponentials(k, 1 if k == 0 else None)
            if valid(k - 1):
                quantise(k - 1)
            if valid(k + 4):
                copy_transposed(k + 4)
            for j in range(CHUNK_TILES):
                for chunk in range(CHUNKS):
                    last_step = (chunk + 1) * STEPS_PER_CHUNK - 1
                    delay = 1 if (chunk, j) == (CHUNKS - 3, 0) else j
                    if k == last_step + 2 + delay:
                        store_tile(chunk, j)
